import numpy as np
import ml_dtypes


def mxq(x, axis, fmt="e4m3"):
    dtype, down = {"e4m3": (ml_dtypes.float8_e4m3fn, 7), "e5m2": (ml_dtypes.float8_e5m2, 14)}[fmt]
    v = np.moveaxis(np.asarray(x, np.float32).astype(ml_dtypes.bfloat16).astype(np.float64), axis, -1)
    blocks = v.reshape(v.shape[:-1] + (-1, 32))
    amax = np.abs(blocks).max(-1, keepdims=True)
    byte = np.maximum(np.where(amax > 0, np.frexp(amax)[1] - 1 + 127, 0) - down, 1)
    scale = np.exp2(byte - 127.0)
    codes = (blocks / scale).astype(np.float32).astype(dtype).astype(np.float64)
    return np.moveaxis((codes * scale).reshape(v.shape), -1, axis)


WIDE = False


def mx_kscale(k):
    if not WIDE:
        return np.ones(k)
    levels = np.array([10, -10, 5, -5, 0])
    a = np.random.permutation(np.resize(levels, k // 512 * 4)).reshape(k // 512, 4)
    idx = np.arange(k)
    return np.exp2(a[idx // 512, idx % 128 // 32])


BF16 = ml_dtypes.bfloat16


def bf(x):
    return np.asarray(x, np.float32).astype(BF16)


def f64(x):
    return np.asarray(x).astype(np.float64)


B, N, D, E = 2, 2048, 4096, 128

EPS = 1e-6
NUM_ITERS = 8
TEMPERATURE = 1.0
FRAC = 0.7
SEP = 2.0


def logsumexp(t, axis):
    m = t.max(axis=axis, keepdims=True)
    return m + np.log(np.exp(t - m).sum(axis=axis, keepdims=True))


def sinkhorn(t):
    t = np.log(np.maximum(t, EPS))
    t = t / TEMPERATURE
    for _ in range(NUM_ITERS):
        t = t - logsumexp(t, -2)
        t = t - logsumexp(t, -1)
    return np.exp(t)


def setup_inputs():
    s = mx_kscale(D)
    p = np.where(np.random.random(D) < 0.5, 1.0, -1.0)
    side = np.where(np.random.random((B, N, 1)) < FRAC, 1.0, -1.0)
    half = np.where(np.arange(E) < E // 2, 1.0, -1.0)[:, None]
    z = np.random.standard_normal((B, N, D))
    z = z - (z @ p)[..., None] * p / D
    g = np.random.standard_normal((E, D))
    g = g - (g @ p)[:, None] * p / D
    return {"x": bf((z + side * p) * s), "w_gate": bf((g / np.sqrt(D) + SEP * half * p / D) / s)}


def reference(x, w_gate):
    gates = mxq(f64(x), 2, "e4m3") @ mxq(f64(w_gate), 1, "e4m3").T
    return sinkhorn(gates)

@@ -1,0 +1,278 @@
+from contextlib import ExitStack
+
+import concourse.mybir as mybir
+from concourse.masks import make_identity
+
+F32 = mybir.dt.float32
+BF16 = mybir.dt.bfloat16
+U32 = mybir.dt.uint32
+U8 = mybir.dt.uint8
+FP8X4 = mybir.dt.float8_e4m3fn_x4
+ALU = mybir.AluOpType
+ACT = mybir.ActivationFunctionType
+AX = mybir.AxisListType
+
+P = 128
+NB = 2
+NTOK = 2048
+D = 4096
+E = 128
+EPS = 1e-6
+ROUNDS = 8
+T = NTOK // P
+PASSES = D // 512
+UNIT_T = 2
+UNIT_N = UNIT_T * P
+UNITS_B = T // UNIT_T
+NU = NB * UNITS_B
+XBUFS = 5
+RING = 5
+FLOPS = 2 * NB * NTOK * D * E
+
+
+def tile_sinkhornrouter_kernel(tc, x, w_gate, out):
+    nc = tc.nc
+    with ExitStack() as ctx:
+        const = ctx.enter_context(tc.tile_pool(name="const", bufs=1))
+        psum = ctx.enter_context(tc.psum_pool(name="psum", bufs=1))
+        xpool = ctx.enter_context(tc.tile_pool(name="xpool", bufs=XBUFS))
+        gpool = ctx.enter_context(tc.tile_pool(name="gpool", bufs=3))
+        cpool = ctx.enter_context(tc.tile_pool(name="cpool", bufs=3))
+        kpool = ctx.enter_context(tc.tile_pool(name="kpool", bufs=3))
+        sink = ctx.enter_context(tc.tile_pool(name="sink", bufs=1))
+
+        def bank(k, shape, name):
+            return psum.tile(shape, F32, tag="bank%d" % k, name=name)
+
+        ident = const.tile([P, P], F32, name="ident")
+        make_identity(nc, ident[:])
+        w_codes = const.tile([P, PASSES * E], U32, name="w_codes", align_bytes=64)
+        w_scales = const.tile([P, PASSES * E], U8, name="w_scales", align_bytes=64)
+
+        x_flat = [x[b].rearrange("(p t) d -> p (t d)", t=T) for b in range(NB)]
+        out_flat = [out[b].rearrange("(p t) e -> p (t e)", t=T) for b in range(NB)]
+
+        x_sb = {}
+        grp = {}
+        xc = {}
+        xs = {}
+        acc = {}
+        kf = {}
+        kt = {}
+
+        def load(i):
+            b, j2 = divmod(i, UNITS_B)
+            x_sb[i] = xpool.tile([P, UNIT_T * D], BF16, name="x_sb")
+            nc.sync.dma_start(
+                out=x_sb[i][:],
+                in_=x_flat[b][:, j2 * UNIT_T * D : (j2 + 1) * UNIT_T * D],
+            )
+
+        with tc.tile_pool(name="wtmp", bufs=1) as wtmp:
+            w_sb = wtmp.tile([P, D], BF16, name="w_sb")
+            nc.sync.dma_start(out=w_sb[:], in_=w_gate)
+            for i in range(XBUFS):
+                load(i)
+            ww = w_sb[:].bitcast(F32)
+            wgrp = wtmp.tile([P, PASSES * E * 4], BF16, name="wgrp", align_bytes=64)
+            wgw = wgrp[:].bitcast(F32).rearrange("p (g e u) -> p g e u", g=PASSES, e=E, u=2)
+            for q in range(PASSES // 2):
+                wt = bank(q % RING, [P, 2, 2, E], "wt")
+                for g2 in range(2):
+                    for u in range(2):
+                        blk = 2 * (2 * q + g2) + u
+                        nc.tensor.transpose(
+                            wt[:, g2, u, :], ww[:, blk * P : (blk + 1) * P], ident[:]
+                        )
+                nc.vector.tensor_copy(
+                    out=wgw[:, 2 * q : 2 * q + 2, :, :],
+                    in_=wt[:].rearrange("p g u e -> p g e u"),
+                )
+            nc.vector.quantize_mx(
+                out=w_codes[:].bitcast(FP8X4), scales=w_scales[:], in_=wgrp[:]
+            )
+
+        k_hi = [sink.tile([P, NTOK], BF16, name="k_hi%d" % b) for b in range(NB)]
+        k_lo = [sink.tile([P, NTOK], BF16, name="k_lo%d" % b) for b in range(NB)]
+        kt_hi = [sink.tile([P, NTOK], BF16, name="kt_hi%d" % b) for b in range(NB)]
+        kt_lo = [sink.tile([P, NTOK], BF16, name="kt_lo%d" % b) for b in range(NB)]
+        kt_f = [sink.tile([P, NTOK], F32, name="kt_f%d" % b) for b in range(NB)]
+        asum = [sink.tile([P, 4], F32, name="asum%d" % b) for b in range(NB)]
+        s_v = [sink.tile([P, 1], F32, name="s_v%d" % b) for b in range(NB)]
+        v_f = [sink.tile([P, 1], F32, name="v_f%d" % b) for b in range(NB)]
+        v_2 = [sink.tile([P, 2], BF16, name="v_2%d" % b) for b in range(NB)]
+        s_u = [sink.tile([P, T], F32, name="s_u%d" % b) for b in range(NB)]
+        u_f = [sink.tile([P, T], F32, name="u_f%d" % b) for b in range(NB)]
+        u_2 = [sink.tile([P, 2, T], BF16, name="u_2%d" % b) for b in range(NB)]
+
+        def transposes(i, g):
+            k = i * PASSES + g
+            if g % 4 == 0:
+                grp[(i, g // 4)] = gpool.tile([P, 4 * UNIT_N * 4], BF16, name="grp", align_bytes=64)
+            xt = bank(k % RING, [P, 2, UNIT_N], "xt")
+            xw = x_sb[i][:].bitcast(F32)
+            for u in range(2):
+                for tl in range(UNIT_T):
+                    c0 = tl * (D // 2) + 256 * g + P * u
+                    nc.tensor.transpose(
+                        xt[:, u, tl * P : (tl + 1) * P], xw[:, c0 : c0 + P], ident[:]
+                    )
+            gw = grp[(i, g // 4)][:].bitcast(F32).rearrange(
+                "p (g n u) -> p g n u", g=4, n=UNIT_N, u=2
+            )
+            src = xt[:].rearrange("p u n -> p n u")
+            if g == 7 or (g == 3 and i % 2 == 1):
+                nc.vector.tensor_copy(out=gw[:, g % 4, :, :], in_=src)
+            else:
+                nc.scalar.copy(out=gw[:, g % 4, :, :], in_=src)
+
+        def quantise(i, h):
+            if h == 0:
+                xc[i] = cpool.tile([P, PASSES * UNIT_N], U32, name="xc", align_bytes=64)
+                xs[i] = cpool.tile([P, PASSES * UNIT_N], U8, name="xs", align_bytes=64)
+            w4 = 4 * UNIT_N
+            nc.vector.quantize_mx(
+                out=xc[i][:, h * w4 : (h + 1) * w4].bitcast(FP8X4),
+                scales=xs[i][:, h * w4 : (h + 1) * w4],
+                in_=grp[(i, h)][:],
+            )
+
+        def passes(i):
+            j = i // 2
+            if i % 2 == 0:
+                acc[j] = bank(RING + j % 2, [P, 2 * UNIT_N], "acc")
+            c0 = (i % 2) * UNIT_N
+            for g in range(PASSES):
+                nc.tensor.matmul_mx(
+                    out=acc[j][:, c0 : c0 + UNIT_N],
+                    lhsT=w_codes[:, g * E : (g + 1) * E].bitcast(FP8X4),
+                    lhsT_scale=w_scales[:, g * E : (g + 1) * E],
+                    rhs=xc[i][:, g * UNIT_N : (g + 1) * UNIT_N].bitcast(FP8X4),
+                    rhs_scale=xs[i][:, g * UNIT_N : (g + 1) * UNIT_N],
+                    start=(g == 0),
+                    stop=(g == PASSES - 1),
+                )
+
+        def setup_a(j):
+            b, jb = divmod(j, 4)
+            cols = slice(jb * 512, (jb + 1) * 512)
+            kf[j] = kpool.tile([P, 512], F32, name="kf")
+            nc.vector.tensor_scalar_max(out=kf[j][:], in0=acc[j][:], scalar1=EPS)
+            nc.scalar.activation(
+                out=k_hi[b][:, cols], in_=kf[j][:], func=ACT.Copy,
+                accum_out=asum[b][:, jb : jb + 1],
+            )
+            nc.vector.tensor_tensor(
+                out=k_lo[b][:, cols], in0=kf[j][:], in1=k_hi[b][:, cols], op=ALU.subtract
+            )
+
+        def setup_t(j):
+            kt[j] = bank(7, [P, 512], "kt")
+            for tl in range(4):
+                nc.tensor.transpose(
+                    kt[j][:, tl * P : (tl + 1) * P], kf[j][:, tl * P : (tl + 1) * P], ident[:]
+                )
+
+        def setup_b(j):
+            b, jb = divmod(j, 4)
+            cols = slice(jb * 512, (jb + 1) * 512)
+            nc.scalar.copy(out=kt_f[b][:, cols], in_=kt[j][:])
+            nc.scalar.copy(out=kt_hi[b][:, cols], in_=kt[j][:])
+            nc.vector.tensor_tensor(
+                out=kt_lo[b][:, cols], in0=kt[j][:], in1=kt_hi[b][:, cols], op=ALU.subtract
+            )
+
+        for i in range(NU + 1):
+            for g in range(PASSES):
+                if i < NU:
+                    transposes(i, g)
+                if g == 1 and i >= 1:
+                    quantise(i - 1, 1)
+                if g == 3 and i >= 1:
+                    passes(i - 1)
+                if g == 5 and i < NU:
+                    quantise(i, 0)
+                if i >= 2 and i % 2 == 0:
+                    if g == 4:
+                        setup_a((i - 2) // 2)
+                    if g == 6:
+                        setup_t((i - 2) // 2)
+                    if g == 7:
+                        setup_b((i - 2) // 2)
+            if i + XBUFS < NU:
+                load(i + XBUFS)
+
+        def split_recip(total, full, pair_hi, pair_lo):
+            with nc.allow_low_precision(reason="upper half of a two-term bf16 split"):
+                nc.vector.reciprocal(out=pair_hi, in_=total)
+            nc.vector.reciprocal(out=full, in_=total)
+            nc.vector.tensor_tensor(out=pair_lo, in0=full, in1=pair_hi, op=ALU.subtract)
+
+        def col_step(b, r):
+            if r == 0:
+                src = asum[b][:]
+            else:
+                ps_a = bank(2 * b, [P, 2], "ps_a")
+                for t in range(T):
+                    for n, part in enumerate((kt_hi[b], kt_lo[b])):
+                        nc.tensor.matmul(
+                            out=ps_a[:],
+                            lhsT=part[:, t * P : (t + 1) * P],
+                            rhs=u_2[b][:, :, t],
+                            start=(t == 0 and n == 0),
+                            stop=(t == T - 1 and n == 1),
+                        )
+                src = ps_a[:]
+            nc.vector.tensor_reduce(out=s_v[b][:], in_=src, axis=AX.X, op=ALU.add)
+            split_recip(s_v[b][:], v_f[b][:], v_2[b][:, 0:1], v_2[b][:, 1:2])
+
+        def row_step(b):
+            ps_b = bank(2 * b + 1, [P, T, 2], "ps_b")
+            for t in range(T):
+                for n, part in enumerate((k_hi[b], k_lo[b])):
+                    nc.tensor.matmul(
+                        out=ps_b[:, t, :],
+                        lhsT=part[:, t * P : (t + 1) * P],
+                        rhs=v_2[b][:],
+                        start=(n == 0),
+                        stop=(n == 1),
+                    )
+            nc.vector.tensor_reduce(out=s_u[b][:], in_=ps_b[:], axis=AX.X, op=ALU.add)
+            split_recip(s_u[b][:], u_f[b][:], u_2[b][:, 0, :], u_2[b][:, 1, :])
+
+        for r in range(ROUNDS):
+            for b in range(NB):
+                col_step(b, r)
+            for b in range(NB):
+                row_step(b)
+
+        for b in range(NB):
+            ps_v = bank(4 + b, [P, E], "ps_v")
+            nc.tensor.matmul(
+                out=ps_v[:], lhsT=v_f[b][:, 0:1].to_broadcast([P, P]), rhs=ident[:],
+                start=True, stop=True,
+            )
+            k3 = kt_f[b][:].rearrange("p (t e) -> p t e", e=E)
+            for q in range(4):
+                nc.vector.tensor_tensor(
+                    out=k3[:, 4 * q : 4 * q + 4, :],
+                    in0=k3[:, 4 * q : 4 * q + 4, :],
+                    in1=ps_v[:].unsqueeze(1).to_broadcast([P, 4, E]),
+                    op=ALU.mult,
+                )
+            for t in range(T):
+                cols = slice(t * E, (t + 1) * E)
+                if t % 3 == 2:
+                    nc.scalar.activation(
+                        out=kt_f[b][:, cols], in_=kt_f[b][:, cols], func=ACT.Copy,
+                        scale=u_f[b][:, t : t + 1],
+                    )
+                else:
+                    nc.vector.tensor_scalar_mul(
+                        out=kt_f[b][:, cols], in0=kt_f[b][:, cols], scalar1=u_f[b][:, t : t + 1]
+                    )
+                if t % 8 == 7:
+                    c0 = (t - 7) * E
+                    nc.sync.dma_start(
+                        out=out_flat[b][:, c0 : c0 + 8 * E], in_=kt_f[b][:, c0 : c0 + 8 * E]
+                    )

@@ -18,27 +18,32 @@ NTOK = 2048
 D = 4096
 E = 128
 EPS = 1e-6
-ROUNDS = 8
 T = NTOK // P
 PASSES = D // 512
 UNIT_T = 2
 UNIT_N = UNIT_T * P
 UNITS_B = T // UNIT_T
 NU = NB * UNITS_B
-XBUFS = 5
+XBUFS = 6
 RING = 5
+NP = 13
+WS = NP + 1
+NDUMMY = 1
+NDUMMY_LONE = 1
+LEAD = 2
+HALF_STEPS = 16
 FLOPS = 2 * NB * NTOK * D * E
 
 
 def tile_sinkhornrouter_kernel(tc, x, w_gate, out):
     nc = tc.nc
     with ExitStack() as ctx:
+        ctx.enter_context(tc.manual_schedule())
         const = ctx.enter_context(tc.tile_pool(name="const", bufs=1))
         psum = ctx.enter_context(tc.psum_pool(name="psum", bufs=1))
         xpool = ctx.enter_context(tc.tile_pool(name="xpool", bufs=XBUFS))
         gpool = ctx.enter_context(tc.tile_pool(name="gpool", bufs=3))
         cpool = ctx.enter_context(tc.tile_pool(name="cpool", bufs=3))
-        kpool = ctx.enter_context(tc.tile_pool(name="kpool", bufs=3))
         sink = ctx.enter_context(tc.tile_pool(name="sink", bufs=1))
 
         def bank(k, shape, name):
@@ -50,6 +55,7 @@ def tile_sinkhornrouter_kernel(tc, x, w_gate, out):
         w_scales = const.tile([P, PASSES * E], U8, name="w_scales", align_bytes=64)
 
         x_flat = [x[b].rearrange("(p t) d -> p (t d)", t=T) for b in range(NB)]
+        x_3d = [x[b].rearrange("(p t) d -> p t d", t=T) for b in range(NB)]
         out_flat = [out[b].rearrange("(p t) e -> p (t e)", t=T) for b in range(NB)]
 
         x_sb = {}
@@ -57,16 +63,43 @@ def tile_sinkhornrouter_kernel(tc, x, w_gate, out):
         xc = {}
         xs = {}
         acc = {}
-        kf = {}
         kt = {}
 
         def load(i):
             b, j2 = divmod(i, UNITS_B)
             x_sb[i] = xpool.tile([P, UNIT_T * D], BF16, name="x_sb")
-            nc.sync.dma_start(
-                out=x_sb[i][:],
-                in_=x_flat[b][:, j2 * UNIT_T * D : (j2 + 1) * UNIT_T * D],
-            )
+            if i < NU - 1:
+                nc.sync.dma_start(
+                    out=x_sb[i][:],
+                    in_=x_flat[b][:, j2 * UNIT_T * D : (j2 + 1) * UNIT_T * D],
+                )
+            else:
+                dst = x_sb[i][:].rearrange("p (t d) -> p t d", t=UNIT_T)
+                for h in range(2):
+                    nc.sync.dma_start(
+                        out=dst[:, :, h * (D // 2) : (h + 1) * (D // 2)],
+                        in_=x_3d[b][:, j2 * UNIT_T : (j2 + 1) * UNIT_T, h * (D // 2) : (h + 1) * (D // 2)],
+                    )
+
+        k_f = [sink.tile([P, NTOK], F32, name="k_f%d" % b) for b in range(NB)]
+        k_hi = [sink.tile([P, NTOK], BF16, name="k_hi%d" % b) for b in range(NB)]
+        k_lo = [sink.tile([P, NTOK], BF16, name="k_lo%d" % b) for b in range(NB)]
+        kt_hi = [sink.tile([P, NTOK], BF16, name="kt_hi%d" % b) for b in range(NB)]
+        kt_lo = [sink.tile([P, NTOK], BF16, name="kt_lo%d" % b) for b in range(NB)]
+        asum = [sink.tile([P, 4], F32, name="asum%d" % b) for b in range(NB)]
+        s_v = [sink.tile([P, 1], F32, name="s_v%d" % b) for b in range(NB)]
+        v_f = [sink.tile([P, 1], F32, name="v_f%d" % b) for b in range(NB)]
+        v_l = [sink.tile([P, WS], BF16, name="v_l%d" % b) for b in range(NB)]
+        v_h = [sink.tile([P, WS], BF16, name="v_h%d" % b) for b in range(NB)]
+        s_u = [sink.tile([P, T], F32, name="s_u%d" % b) for b in range(NB)]
+        u_f = [sink.tile([P, T], F32, name="u_f%d" % b) for b in range(NB)]
+        u_l = [sink.tile([P, T, WS], BF16, name="u_l%d" % b) for b in range(NB)]
+        u_h = [sink.tile([P, T, WS], BF16, name="u_h%d" % b) for b in range(NB)]
+        for b in range(NB):
+            nc.vector.memset(v_l[b][:], 0.0)
+            nc.vector.memset(v_h[b][:], 0.0)
+            nc.vector.memset(u_l[b][:], 0.0)
+            nc.vector.memset(u_h[b][:], 0.0)
 
         with tc.tile_pool(name="wtmp", bufs=1) as wtmp:
             w_sb = wtmp.tile([P, D], BF16, name="w_sb")
@@ -84,29 +117,18 @@ def tile_sinkhornrouter_kernel(tc, x, w_gate, out):
                         nc.tensor.transpose(
                             wt[:, g2, u, :], ww[:, blk * P : (blk + 1) * P], ident[:]
                         )
-                nc.vector.tensor_copy(
-                    out=wgw[:, 2 * q : 2 * q + 2, :, :],
-                    in_=wt[:].rearrange("p g u e -> p g e u"),
-                )
+                dst = wgw[:, 2 * q : 2 * q + 2, :, :]
+                src = wt[:].rearrange("p g u e -> p g e u")
+                if q % 2 == 0:
+                    nc.vector.tensor_copy(out=dst, in_=src)
+                else:
+                    nc.scalar.copy(out=dst, in_=src)
             nc.vector.quantize_mx(
                 out=w_codes[:].bitcast(FP8X4), scales=w_scales[:], in_=wgrp[:]
             )
 
-        k_hi = [sink.tile([P, NTOK], BF16, name="k_hi%d" % b) for b in range(NB)]
-        k_lo = [sink.tile([P, NTOK], BF16, name="k_lo%d" % b) for b in range(NB)]
-        kt_hi = [sink.tile([P, NTOK], BF16, name="kt_hi%d" % b) for b in range(NB)]
-        kt_lo = [sink.tile([P, NTOK], BF16, name="kt_lo%d" % b) for b in range(NB)]
-        kt_f = [sink.tile([P, NTOK], F32, name="kt_f%d" % b) for b in range(NB)]
-        asum = [sink.tile([P, 4], F32, name="asum%d" % b) for b in range(NB)]
-        s_v = [sink.tile([P, 1], F32, name="s_v%d" % b) for b in range(NB)]
-        v_f = [sink.tile([P, 1], F32, name="v_f%d" % b) for b in range(NB)]
-        v_2 = [sink.tile([P, 2], BF16, name="v_2%d" % b) for b in range(NB)]
-        s_u = [sink.tile([P, T], F32, name="s_u%d" % b) for b in range(NB)]
-        u_f = [sink.tile([P, T], F32, name="u_f%d" % b) for b in range(NB)]
-        u_2 = [sink.tile([P, 2, T], BF16, name="u_2%d" % b) for b in range(NB)]
-
         def transposes(i, g):
-            k = i * PASSES + g
+            k = i * PASSES + g + 4
             if g % 4 == 0:
                 grp[(i, g // 4)] = gpool.tile([P, 4 * UNIT_N * 4], BF16, name="grp", align_bytes=64)
             xt = bank(k % RING, [P, 2, UNIT_N], "xt")
@@ -121,28 +143,30 @@ def tile_sinkhornrouter_kernel(tc, x, w_gate, out):
                 "p (g n u) -> p g n u", g=4, n=UNIT_N, u=2
             )
             src = xt[:].rearrange("p u n -> p n u")
-            if g == 7 or (g == 3 and i % 2 == 1):
+            if g == 6 or (g == 2 and i % 2 == 1):
                 nc.vector.tensor_copy(out=gw[:, g % 4, :, :], in_=src)
             else:
                 nc.scalar.copy(out=gw[:, g % 4, :, :], in_=src)
 
-        def quantise(i, h):
-            if h == 0:
+        def quantise(i, g0, n):
+            if g0 == 0:
                 xc[i] = cpool.tile([P, PASSES * UNIT_N], U32, name="xc", align_bytes=64)
                 xs[i] = cpool.tile([P, PASSES * UNIT_N], U8, name="xs", align_bytes=64)
-            w4 = 4 * UNIT_N
+            c0 = g0 * UNIT_N
+            c1 = (g0 + n) * UNIT_N
+            r0 = (g0 % 4) * UNIT_N * 4
             nc.vector.quantize_mx(
-                out=xc[i][:, h * w4 : (h + 1) * w4].bitcast(FP8X4),
-                scales=xs[i][:, h * w4 : (h + 1) * w4],
-                in_=grp[(i, h)][:],
+                out=xc[i][:, c0:c1].bitcast(FP8X4),
+                scales=xs[i][:, c0:c1],
+                in_=grp[(i, g0 // 4)][:, r0 : r0 + n * UNIT_N * 4],
             )
 
-        def passes(i):
+        def passes(i, g0, n):
             j = i // 2
-            if i % 2 == 0:
+            if i % 2 == 0 and g0 == 0:
                 acc[j] = bank(RING + j % 2, [P, 2 * UNIT_N], "acc")
             c0 = (i % 2) * UNIT_N
-            for g in range(PASSES):
+            for g in range(g0, g0 + n):
                 nc.tensor.matmul_mx(
                     out=acc[j][:, c0 : c0 + UNIT_N],
                     lhsT=w_codes[:, g * E : (g + 1) * E].bitcast(FP8X4),
@@ -153,126 +177,253 @@ def tile_sinkhornrouter_kernel(tc, x, w_gate, out):
                     stop=(g == PASSES - 1),
                 )
 
-        def setup_a(j):
+        def where(j):
             b, jb = divmod(j, 4)
-            cols = slice(jb * 512, (jb + 1) * 512)
-            kf[j] = kpool.tile([P, 512], F32, name="kf")
-            nc.vector.tensor_scalar_max(out=kf[j][:], in0=acc[j][:], scalar1=EPS)
+            return b, jb, slice(jb * 512, (jb + 1) * 512)
+
+        def su_a(j):
+            b, jb, cols = where(j)
+            nc.vector.tensor_scalar_max(out=k_f[b][:, cols], in0=acc[j][:], scalar1=EPS)
+
+        def su_b(j):
+            b, jb, cols = where(j)
             nc.scalar.activation(
-                out=k_hi[b][:, cols], in_=kf[j][:], func=ACT.Copy,
+                out=k_hi[b][:, cols], in_=k_f[b][:, cols], func=ACT.Copy,
                 accum_out=asum[b][:, jb : jb + 1],
             )
+
+        def su_c(j):
+            b, jb, cols = where(j)
             nc.vector.tensor_tensor(
-                out=k_lo[b][:, cols], in0=kf[j][:], in1=k_hi[b][:, cols], op=ALU.subtract
+                out=k_lo[b][:, cols], in0=k_f[b][:, cols], in1=k_hi[b][:, cols], op=ALU.subtract
             )
 
-        def setup_t(j):
+        def su_t(j):
+            b, jb, cols = where(j)
             kt[j] = bank(7, [P, 512], "kt")
             for tl in range(4):
-                nc.tensor.transpose(
-                    kt[j][:, tl * P : (tl + 1) * P], kf[j][:, tl * P : (tl + 1) * P], ident[:]
-                )
+                c0 = jb * 512 + tl * P
+                nc.tensor.transpose(kt[j][:, tl * P : (tl + 1) * P], k_f[b][:, c0 : c0 + P], ident[:])
 
-        def setup_b(j):
-            b, jb = divmod(j, 4)
-            cols = slice(jb * 512, (jb + 1) * 512)
-            nc.scalar.copy(out=kt_f[b][:, cols], in_=kt[j][:])
+        def su_f(j):
+            b, jb, cols = where(j)
             nc.scalar.copy(out=kt_hi[b][:, cols], in_=kt[j][:])
+
+        def su_g(j):
+            b, jb, cols = where(j)
             nc.vector.tensor_tensor(
                 out=kt_lo[b][:, cols], in0=kt[j][:], in1=kt_hi[b][:, cols], op=ALU.subtract
             )
 
-        for i in range(NU + 1):
+        BANK_B = (3, 0)
+        BANK_A = (4, 1)
+        FIN = ((2, 6, 7, 3), (4, 1, 2, 6))
+        ps = {}
+
+        def thin(dst, part, t, rhs, start, stop):
+            nc.tensor.matmul(
+                out=dst, lhsT=part[:, t * P : (t + 1) * P], rhs=rhs, start=start, stop=stop
+            )
+
+        def late(b, k):
+            return range(12, T) if (b == 1 and k == 1) else range(0)
+
+        def pe_lo(b, k):
+            if k % 2 == 1:
+                pb = bank(BANK_B[b], [P, T, 2 * NP], "ps_b")
+                ps[("b", b)] = pb
+                for t in range(T):
+                    if t not in late(b, k):
+                        thin(pb[:, t, 0:NP], k_lo[b], t, v_l[b][:, 0:NP], True, True)
+            else:
+                pa = bank(BANK_A[b], [P, 2 * NP], "ps_a")
+                ps[("a", b)] = pa
+                for t in range(T):
+                    thin(pa[:, 0:NP], kt_lo[b], t, u_l[b][:, t, 0:NP], t == 0, t == T - 1)
+
+        def pe_hi(b, k):
+            if k % 2 == 1:
+                pb = ps[("b", b)]
+                for t in range(T):
+                    thin(pb[:, t, NP : 2 * NP], k_hi[b], t, v_h[b][:, 0:NP], True, True)
+                for t in late(b, k):
+                    thin(pb[:, t, 0:NP], k_lo[b], t, v_l[b][:, 0:NP], True, True)
+            else:
+                pa = ps[("a", b)]
+                for t in range(T):
+                    thin(pa[:, NP : 2 * NP], kt_hi[b], t, u_h[b][:, t, 0:NP], t == 0, t == T - 1)
+
+        def pe_part(b, k):
+            pe_lo(b, k)
+            pe_hi(b, k)
+
+        def v_part(b, k):
+            if k % 2 == 0:
+                if k == 0:
+                    nc.vector.tensor_reduce(out=s_v[b][:], in_=asum[b][:], axis=AX.X, op=ALU.add)
+                    first = s_v[b][:]
+                else:
+                    first = ps[("a", b)][:, NP : NP + 1]
+                total, full = s_v[b][:], v_f[b][:]
+                hi_l, hi_h, lo_h = v_l[b][:, NP - 1 : NP], v_h[b][:, 0:1], v_h[b][:, 1:2]
+                whole = None if k == 0 else ps[("a", b)][:, NP - 1 : NP + 2]
+            else:
+                first = ps[("b", b)][:, :, NP]
+                total, full = s_u[b][:], u_f[b][:]
+                hi_l, hi_h, lo_h = u_l[b][:, :, NP - 1], u_h[b][:, :, 0], u_h[b][:, :, 1]
+                whole = ps[("b", b)][:, :, NP - 1 : NP + 2]
+            last = k == HALF_STEPS - 1
+            if not last:
+                with nc.allow_low_precision(reason="upper term of a two-term bf16 split"):
+                    nc.vector.reciprocal(out=hi_l, in_=first)
+            if whole is not None:
+                nc.vector.tensor_reduce(out=total, in_=whole, axis=AX.X, op=ALU.add)
+            if not last:
+                nc.vector.tensor_copy(out=hi_h, in_=hi_l)
+            nc.vector.reciprocal(out=full, in_=total)
+            if not last:
+                nc.vector.tensor_tensor(out=lo_h, in0=full, in1=hi_h, op=ALU.subtract)
+
+        dummy = {}
+
+        def dummies(n):
+            if n == 0:
+                return
+            if "t" not in dummy:
+                dummy["t"] = bank(5, [P, 512], "idle")
+            for q in range(n):
+                nc.tensor.matmul_mx(
+                    out=dummy["t"][:],
+                    lhsT=w_codes[:, 0:E].bitcast(FP8X4),
+                    lhsT_scale=w_scales[:, 0:E],
+                    rhs=xc[NU - 1][:, 0:512].bitcast(FP8X4),
+                    rhs_scale=xs[NU - 1][:, 0:512],
+                    start=True,
+                    stop=True,
+                )
+
+        fin = {}
+        k3 = [k_f[b][:].rearrange("p (t e) -> p t e", e=E) for b in range(NB)]
+
+        def times_v(b, q, eng):
+            cols = slice(q * 512, (q + 1) * 512)
+            if eng == "s":
+                nc.scalar.activation(
+                    out=k_f[b][:, cols], in_=k_f[b][:, cols], func=ACT.Copy, scale=v_f[b][:, 0:1]
+                )
+            else:
+                nc.vector.tensor_scalar_mul(
+                    out=k_f[b][:, cols], in0=k_f[b][:, cols], scalar1=v_f[b][:, 0:1]
+                )
+
+        def fin_t(b, q):
+            fin[(b, q)] = bank(FIN[b][q], [P, 4, E], "fin")
+            for tl in range(4):
+                c0 = (4 * q + tl) * P
+                nc.tensor.transpose(fin[(b, q)][:, tl, :], k_f[b][:, c0 : c0 + P], ident[:])
+
+        def times_u(b, q, eng):
+            if eng == "s":
+                for tl in range(4):
+                    t = 4 * q + tl
+                    nc.scalar.activation(
+                        out=k3[b][:, t, :], in_=fin[(b, q)][:, tl, :], func=ACT.Copy,
+                        scale=u_f[b][:, t : t + 1],
+                    )
+            else:
+                nc.vector.tensor_tensor(
+                    out=k3[b][:, 4 * q : 4 * q + 4, :],
+                    in0=fin[(b, q)][:],
+                    in1=u_f[b][:, 4 * q : 4 * q + 4].unsqueeze(2).to_broadcast([P, 4, E]),
+                    op=ALU.mult,
+                )
+
+        def store(b, q, n):
+            nc.sync.dma_start(
+                out=out_flat[b][:, q * 512 : (q + n) * 512], in_=k_f[b][:, q * 512 : (q + n) * 512]
+            )
+
+        for i in range(NU):
+            odd = i % 2 == 1 and i >= 3
+            j = (i - 3) // 2
+            last = i == NU - 1
             for g in range(PASSES):
-                if i < NU:
-                    transposes(i, g)
+                transposes(i, g)
+                if g == 0 and odd:
+                    su_t(j)
+                    su_b(j)
                 if g == 1 and i >= 1:
-                    quantise(i - 1, 1)
+                    quantise(i - 1, 4, 4)
+                if g == 2 and odd:
+                    su_c(j)
                 if g == 3 and i >= 1:
-                    passes(i - 1)
-                if g == 5 and i < NU:
-                    quantise(i, 0)
-                if i >= 2 and i % 2 == 0:
-                    if g == 4:
-                        setup_a((i - 2) // 2)
-                    if g == 6:
-                        setup_t((i - 2) // 2)
-                    if g == 7:
-                        setup_b((i - 2) // 2)
+                    passes(i - 1, 0, PASSES)
+                if g == 3 and odd:
+                    su_f(j)
+                if g == 4 and odd:
+                    su_g(j)
+                if g == 4 and i == 10:
+                    v_part(0, 0)
+                if g == 5:
+                    quantise(i, 0, 4)
+                if g == 6 and i % 2 == 0 and i >= 2:
+                    su_a((i - 2) // 2)
+                if g == 7 and last:
+                    quantise(i, 4, 2)
             if i + XBUFS < NU:
                 load(i + XBUFS)
 
-        def split_recip(total, full, pair_hi, pair_lo):
-            with nc.allow_low_precision(reason="upper half of a two-term bf16 split"):
-                nc.vector.reciprocal(out=pair_hi, in_=total)
-            nc.vector.reciprocal(out=full, in_=total)
-            nc.vector.tensor_tensor(out=pair_lo, in0=full, in1=pair_hi, op=ALU.subtract)
+        JL = NU // 2 - 1
+        passes(NU - 1, 0, 6)
+        pe_part(0, 1)
+        quantise(NU - 1, 6, 2)
+        passes(NU - 1, 6, 2)
+        v_part(0, 1)
+        pe_part(0, 2)
+        su_a(JL)
+        su_b(JL)
+        su_t(JL)
+        v_part(1, 0)
+        su_c(JL)
+        su_f(JL)
+        v_part(0, 2)
+        su_g(JL)
 
-        def col_step(b, r):
-            if r == 0:
-                src = asum[b][:]
-            else:
-                ps_a = bank(2 * b, [P, 2], "ps_a")
-                for t in range(T):
-                    for n, part in enumerate((kt_hi[b], kt_lo[b])):
-                        nc.tensor.matmul(
-                            out=ps_a[:],
-                            lhsT=part[:, t * P : (t + 1) * P],
-                            rhs=u_2[b][:, :, t],
-                            start=(t == 0 and n == 0),
-                            stop=(t == T - 1 and n == 1),
-                        )
-                src = ps_a[:]
-            nc.vector.tensor_reduce(out=s_v[b][:], in_=src, axis=AX.X, op=ALU.add)
-            split_recip(s_v[b][:], v_f[b][:], v_2[b][:, 0:1], v_2[b][:, 1:2])
+        for k in range(1, HALF_STEPS - LEAD):
+            k0 = k + LEAD
+            pe_part(1, k)
+            pe_part(0, k0)
+            dummies(NDUMMY)
+            v_part(1, k)
+            v_part(0, k0)
+            if k0 == HALF_STEPS - 2:
+                for q in range(4):
+                    times_v(0, q, "s")
 
-        def row_step(b):
-            ps_b = bank(2 * b + 1, [P, T, 2], "ps_b")
-            for t in range(T):
-                for n, part in enumerate((k_hi[b], k_lo[b])):
-                    nc.tensor.matmul(
-                        out=ps_b[:, t, :],
-                        lhsT=part[:, t * P : (t + 1) * P],
-                        rhs=v_2[b][:],
-                        start=(n == 0),
-                        stop=(n == 1),
-                    )
-            nc.vector.tensor_reduce(out=s_u[b][:], in_=ps_b[:], axis=AX.X, op=ALU.add)
-            split_recip(s_u[b][:], u_f[b][:], u_2[b][:, 0, :], u_2[b][:, 1, :])
-
-        for r in range(ROUNDS):
-            for b in range(NB):
-                col_step(b, r)
-            for b in range(NB):
-                row_step(b)
-
-        for b in range(NB):
-            ps_v = bank(4 + b, [P, E], "ps_v")
-            nc.tensor.matmul(
-                out=ps_v[:], lhsT=v_f[b][:, 0:1].to_broadcast([P, P]), rhs=ident[:],
-                start=True, stop=True,
-            )
-            k3 = kt_f[b][:].rearrange("p (t e) -> p t e", e=E)
-            for q in range(4):
-                nc.vector.tensor_tensor(
-                    out=k3[:, 4 * q : 4 * q + 4, :],
-                    in0=k3[:, 4 * q : 4 * q + 4, :],
-                    in1=ps_v[:].unsqueeze(1).to_broadcast([P, 4, E]),
-                    op=ALU.mult,
-                )
-            for t in range(T):
-                cols = slice(t * E, (t + 1) * E)
-                if t % 3 == 2:
-                    nc.scalar.activation(
-                        out=kt_f[b][:, cols], in_=kt_f[b][:, cols], func=ACT.Copy,
-                        scale=u_f[b][:, t : t + 1],
-                    )
-                else:
-                    nc.vector.tensor_scalar_mul(
-                        out=kt_f[b][:, cols], in0=kt_f[b][:, cols], scalar1=u_f[b][:, t : t + 1]
-                    )
-                if t % 8 == 7:
-                    c0 = (t - 7) * E
-                    nc.sync.dma_start(
-                        out=out_flat[b][:, c0 : c0 + 8 * E], in_=kt_f[b][:, c0 : c0 + 8 * E]
-                    )
+        pe_part(1, 14)
+        dummies(NDUMMY_LONE)
+        fin_t(0, 0)
+        v_part(1, 14)
+        times_u(0, 0, "s")
+        store(0, 0, 1)
+        times_v(1, 0, "v")
+        times_v(1, 1, "v")
+        times_v(1, 2, "s")
+        times_v(1, 3, "s")
+        pe_lo(1, 15)
+        dummies(NDUMMY_LONE)
+        pe_hi(1, 15)
+        for q in range(1, 4):
+            fin_t(0, q)
+        times_u(0, 1, "s")
+        store(0, 1, 1)
+        times_u(0, 2, "s")
+        store(0, 2, 1)
+        v_part(1, 15)
+        times_u(0, 3, "v")
+        store(0, 3, 1)
+        for q in range(4):
+            fin_t(1, q)
+        for q in range(4):
+            times_u(1, q, "s" if q == 1 else "v")
+            store(1, q, 1)

@@ -143,7 +143,7 @@ def tile_sinkhornrouter_kernel(tc, x, w_gate, out):
                 "p (g n u) -> p g n u", g=4, n=UNIT_N, u=2
             )
             src = xt[:].rearrange("p u n -> p n u")
-            if g == 6 or (g == 2 and i % 2 == 1):
+            if g == 6 or (g == 2 and i % 2 == 0):
                 nc.vector.tensor_copy(out=gw[:, g % 4, :, :], in_=src)
             else:
                 nc.scalar.copy(out=gw[:, g % 4, :, :], in_=src)
@@ -344,40 +344,43 @@ def tile_sinkhornrouter_kernel(tc, x, w_gate, out):
             )
 
         for i in range(NU):
+            even = i % 2 == 0 and i >= 2
             odd = i % 2 == 1 and i >= 3
-            j = (i - 3) // 2
-            last = i == NU - 1
+            j = (i - 2) // 2
             for g in range(PASSES):
                 transposes(i, g)
+                if g == 0 and i >= 1:
+                    quantise(i - 1, 6, 2)
                 if g == 0 and odd:
-                    su_t(j)
-                    su_b(j)
-                if g == 1 and i >= 1:
-                    quantise(i - 1, 4, 4)
-                if g == 2 and odd:
-                    su_c(j)
-                if g == 3 and i >= 1:
-                    passes(i - 1, 0, PASSES)
-                if g == 3 and odd:
                     su_f(j)
-                if g == 4 and odd:
+                    su_c(j)
+                if g == 1:
+                    quantise(i, 0, 2)
+                if g == 3 and i >= 1:
+                    passes(i - 1, 4, 4)
+                if g == 3 and even:
+                    su_a(j)
+                if g == 3 and odd:
                     su_g(j)
-                if g == 4 and i == 10:
+                if g == 3 and i == 10:
                     v_part(0, 0)
-                if g == 5:
-                    quantise(i, 0, 4)
-                if g == 6 and i % 2 == 0 and i >= 2:
-                    su_a((i - 2) // 2)
-                if g == 7 and last:
+                if g == 3:
+                    quantise(i, 2, 2)
+                if g == 5 and even:
+                    su_b(j)
+                if g == 6:
                     quantise(i, 4, 2)
+                if g == 7 and even:
+                    su_t(j)
+                if g == 7:
+                    passes(i, 0, 4)
             if i + XBUFS < NU:
                 load(i + XBUFS)
 
         JL = NU // 2 - 1
-        passes(NU - 1, 0, 6)
         pe_part(0, 1)
         quantise(NU - 1, 6, 2)
-        passes(NU - 1, 6, 2)
+        passes(NU - 1, 4, 4)
         v_part(0, 1)
         pe_part(0, 2)
         su_a(JL)

@@ -273,16 +273,15 @@ def tile_sinkhornrouter_kernel(tc, x, w_gate, out):
                 hi_l, hi_h, lo_h = u_l[b][:, :, NP - 1], u_h[b][:, :, 0], u_h[b][:, :, 1]
                 whole = ps[("b", b)][:, :, NP - 1 : NP + 2]
             last = k == HALF_STEPS - 1
-            if not last:
-                with nc.allow_low_precision(reason="upper term of a two-term bf16 split"):
-                    nc.vector.reciprocal(out=hi_l, in_=first)
             if whole is not None:
                 nc.vector.tensor_reduce(out=total, in_=whole, axis=AX.X, op=ALU.add)
             if not last:
-                nc.vector.tensor_copy(out=hi_h, in_=hi_l)
+                with nc.allow_low_precision(reason="upper term of a two-term bf16 split"):
+                    nc.vector.reciprocal(out=hi_l, in_=first)
             nc.vector.reciprocal(out=full, in_=total)
             if not last:
-                nc.vector.tensor_tensor(out=lo_h, in0=full, in1=hi_h, op=ALU.subtract)
+                nc.vector.tensor_copy(out=hi_h, in_=hi_l)
+                nc.vector.tensor_tensor(out=lo_h, in0=full, in1=hi_l, op=ALU.subtract)
 
         dummy = {}
 
@@ -386,6 +385,7 @@ def tile_sinkhornrouter_kernel(tc, x, w_gate, out):
         su_a(JL)
         su_b(JL)
         su_t(JL)
+        dummies(2)
         v_part(1, 0)
         su_c(JL)
         su_f(JL)
@@ -395,6 +395,7 @@ def tile_sinkhornrouter_kernel(tc, x, w_gate, out):
         for k in range(1, HALF_STEPS - LEAD):
             k0 = k + LEAD
             pe_part(1, k)
+            dummies(NDUMMY)
             pe_part(0, k0)
             dummies(NDUMMY)
             v_part(1, k)

@@ -30,6 +30,9 @@ NP = 13
 WS = NP + 1
 NDUMMY = 1
 NDUMMY_LONE = 1
+ZP = 2
+WARM = 12
+BRIDGE = 2
 LEAD = 2
 HALF_STEPS = 16
 FLOPS = 2 * NB * NTOK * D * E
@@ -54,6 +57,24 @@ def tile_sinkhornrouter_kernel(tc, x, w_gate, out):
         w_codes = const.tile([P, PASSES * E], U32, name="w_codes", align_bytes=64)
         w_scales = const.tile([P, PASSES * E], U8, name="w_scales", align_bytes=64)
 
+        z_codes = const.tile([P, 512], U32, name="z_codes", align_bytes=64)
+        z_scales = const.tile([P, 512], U8, name="z_scales", align_bytes=64)
+        with tc.tile_pool(name="ztmp", bufs=1) as ztmp:
+            z_in = ztmp.tile([P, 2048], BF16, name="z_in", align_bytes=64)
+            nc.vector.memset(z_in[:], 0.0)
+            nc.vector.quantize_mx(out=z_codes[:].bitcast(FP8X4), scales=z_scales[:], in_=z_in[:])
+
+        def zero_pass(dst, n, start, stop):
+            nc.tensor.matmul_mx(
+                out=dst,
+                lhsT=z_codes[:, 0:E].bitcast(FP8X4),
+                lhsT_scale=z_scales[:, 0:E],
+                rhs=z_codes[:, 0:n].bitcast(FP8X4),
+                rhs_scale=z_scales[:, 0:n],
+                start=start,
+                stop=stop,
+            )
+
         x_flat = [x[b].rearrange("(p t) d -> p (t d)", t=T) for b in range(NB)]
         x_3d = [x[b].rearrange("(p t) d -> p t d", t=T) for b in range(NB)]
         out_flat = [out[b].rearrange("(p t) e -> p (t e)", t=T) for b in range(NB)]
@@ -68,7 +89,7 @@ def tile_sinkhornrouter_kernel(tc, x, w_gate, out):
         def load(i):
             b, j2 = divmod(i, UNITS_B)
             x_sb[i] = xpool.tile([P, UNIT_T * D], BF16, name="x_sb")
-            if i < NU - 1:
+            if 0 < i < NU - 1:
                 nc.sync.dma_start(
                     out=x_sb[i][:],
                     in_=x_flat[b][:, j2 * UNIT_T * D : (j2 + 1) * UNIT_T * D],
@@ -106,6 +127,9 @@ def tile_sinkhornrouter_kernel(tc, x, w_gate, out):
             nc.sync.dma_start(out=w_sb[:], in_=w_gate)
             for i in range(XBUFS):
                 load(i)
+            warm = bank(6, [P, 512], "warm")
+            for q in range(WARM):
+                zero_pass(warm[:], 512, True, True)
             ww = w_sb[:].bitcast(F32)
             wgrp = wtmp.tile([P, PASSES * E * 4], BF16, name="wgrp", align_bytes=64)
             wgw = wgrp[:].bitcast(F32).rearrange("p (g e u) -> p g e u", g=PASSES, e=E, u=2)
@@ -123,6 +147,9 @@ def tile_sinkhornrouter_kernel(tc, x, w_gate, out):
                     nc.vector.tensor_copy(out=dst, in_=src)
                 else:
                     nc.scalar.copy(out=dst, in_=src)
+                    zero_pass(warm[:], 512, True, True)
+            for q in range(BRIDGE):
+                zero_pass(warm[:], 512, True, True)
             nc.vector.quantize_mx(
                 out=w_codes[:].bitcast(FP8X4), scales=w_scales[:], in_=wgrp[:]
             )
@@ -167,6 +194,9 @@ def tile_sinkhornrouter_kernel(tc, x, w_gate, out):
                 acc[j] = bank(RING + j % 2, [P, 2 * UNIT_N], "acc")
             c0 = (i % 2) * UNIT_N
             for g in range(g0, g0 + n):
+                if g == PASSES - 1:
+                    for q in range(ZP):
+                        zero_pass(acc[j][:, c0 : c0 + UNIT_N], UNIT_N, False, False)
                 nc.tensor.matmul_mx(
                     out=acc[j][:, c0 : c0 + UNIT_N],
                     lhsT=w_codes[:, g * E : (g + 1) * E].bitcast(FP8X4),
@@ -176,6 +206,9 @@ def tile_sinkhornrouter_kernel(tc, x, w_gate, out):
                     start=(g == 0),
                     stop=(g == PASSES - 1),
                 )
+            if g0 + n < PASSES:
+                for q in range(ZP):
+                    zero_pass(acc[j][:, c0 : c0 + UNIT_N], UNIT_N, False, False)
 
         def where(j):
             b, jb = divmod(j, 4)
@@ -291,15 +324,7 @@ def tile_sinkhornrouter_kernel(tc, x, w_gate, out):
             if "t" not in dummy:
                 dummy["t"] = bank(5, [P, 512], "idle")
             for q in range(n):
-                nc.tensor.matmul_mx(
-                    out=dummy["t"][:],
-                    lhsT=w_codes[:, 0:E].bitcast(FP8X4),
-                    lhsT_scale=w_scales[:, 0:E],
-                    rhs=xc[NU - 1][:, 0:512].bitcast(FP8X4),
-                    rhs_scale=xs[NU - 1][:, 0:512],
-                    start=True,
-                    stop=True,
-                )
+                zero_pass(dummy["t"][:], 512, True, True)
 
         fin = {}
         k3 = [k_f[b][:].rearrange("p (t e) -> p t e", e=E) for b in range(NB)]
@@ -355,6 +380,8 @@ def tile_sinkhornrouter_kernel(tc, x, w_gate, out):
                     su_c(j)
                 if g == 1:
                     quantise(i, 0, 2)
+                if g == 3 and i == 0:
+                    zero_pass(warm[:], 512, True, True)
                 if g == 3 and i >= 1:
                     passes(i - 1, 4, 4)
                 if g == 3 and even:

@@ -30,9 +30,6 @@ NP = 13
 WS = NP + 1
 NDUMMY = 1
 NDUMMY_LONE = 1
-ZP = 2
-WARM = 12
-BRIDGE = 2
 LEAD = 2
 HALF_STEPS = 16
 FLOPS = 2 * NB * NTOK * D * E
@@ -57,24 +54,6 @@ def tile_sinkhornrouter_kernel(tc, x, w_gate, out):
         w_codes = const.tile([P, PASSES * E], U32, name="w_codes", align_bytes=64)
         w_scales = const.tile([P, PASSES * E], U8, name="w_scales", align_bytes=64)
 
-        z_codes = const.tile([P, 512], U32, name="z_codes", align_bytes=64)
-        z_scales = const.tile([P, 512], U8, name="z_scales", align_bytes=64)
-        with tc.tile_pool(name="ztmp", bufs=1) as ztmp:
-            z_in = ztmp.tile([P, 2048], BF16, name="z_in", align_bytes=64)
-            nc.vector.memset(z_in[:], 0.0)
-            nc.vector.quantize_mx(out=z_codes[:].bitcast(FP8X4), scales=z_scales[:], in_=z_in[:])
-
-        def zero_pass(dst, n, start, stop):
-            nc.tensor.matmul_mx(
-                out=dst,
-                lhsT=z_codes[:, 0:E].bitcast(FP8X4),
-                lhsT_scale=z_scales[:, 0:E],
-                rhs=z_codes[:, 0:n].bitcast(FP8X4),
-                rhs_scale=z_scales[:, 0:n],
-                start=start,
-                stop=stop,
-            )
-
         x_flat = [x[b].rearrange("(p t) d -> p (t d)", t=T) for b in range(NB)]
         x_3d = [x[b].rearrange("(p t) d -> p t d", t=T) for b in range(NB)]
         out_flat = [out[b].rearrange("(p t) e -> p (t e)", t=T) for b in range(NB)]
@@ -89,7 +68,7 @@ def tile_sinkhornrouter_kernel(tc, x, w_gate, out):
         def load(i):
             b, j2 = divmod(i, UNITS_B)
             x_sb[i] = xpool.tile([P, UNIT_T * D], BF16, name="x_sb")
-            if 0 < i < NU - 1:
+            if i < NU - 1:
                 nc.sync.dma_start(
                     out=x_sb[i][:],
                     in_=x_flat[b][:, j2 * UNIT_T * D : (j2 + 1) * UNIT_T * D],
@@ -127,9 +106,6 @@ def tile_sinkhornrouter_kernel(tc, x, w_gate, out):
             nc.sync.dma_start(out=w_sb[:], in_=w_gate)
             for i in range(XBUFS):
                 load(i)
-            warm = bank(6, [P, 512], "warm")
-            for q in range(WARM):
-                zero_pass(warm[:], 512, True, True)
             ww = w_sb[:].bitcast(F32)
             wgrp = wtmp.tile([P, PASSES * E * 4], BF16, name="wgrp", align_bytes=64)
             wgw = wgrp[:].bitcast(F32).rearrange("p (g e u) -> p g e u", g=PASSES, e=E, u=2)
@@ -147,9 +123,6 @@ def tile_sinkhornrouter_kernel(tc, x, w_gate, out):
                     nc.vector.tensor_copy(out=dst, in_=src)
                 else:
                     nc.scalar.copy(out=dst, in_=src)
-                    zero_pass(warm[:], 512, True, True)
-            for q in range(BRIDGE):
-                zero_pass(warm[:], 512, True, True)
             nc.vector.quantize_mx(
                 out=w_codes[:].bitcast(FP8X4), scales=w_scales[:], in_=wgrp[:]
             )
@@ -194,9 +167,6 @@ def tile_sinkhornrouter_kernel(tc, x, w_gate, out):
                 acc[j] = bank(RING + j % 2, [P, 2 * UNIT_N], "acc")
             c0 = (i % 2) * UNIT_N
             for g in range(g0, g0 + n):
-                if g == PASSES - 1:
-                    for q in range(ZP):
-                        zero_pass(acc[j][:, c0 : c0 + UNIT_N], UNIT_N, False, False)
                 nc.tensor.matmul_mx(
                     out=acc[j][:, c0 : c0 + UNIT_N],
                     lhsT=w_codes[:, g * E : (g + 1) * E].bitcast(FP8X4),
@@ -206,24 +176,22 @@ def tile_sinkhornrouter_kernel(tc, x, w_gate, out):
                     start=(g == 0),
                     stop=(g == PASSES - 1),
                 )
-            if g0 + n < PASSES:
-                for q in range(ZP):
-                    zero_pass(acc[j][:, c0 : c0 + UNIT_N], UNIT_N, False, False)
 
         def where(j):
             b, jb = divmod(j, 4)
             return b, jb, slice(jb * 512, (jb + 1) * 512)
 
-        def su_a(j):
+        def su_a(j, c0, n):
             b, jb, cols = where(j)
-            nc.vector.tensor_scalar_max(out=k_f[b][:, cols], in0=acc[j][:], scalar1=EPS)
+            nc.vector.tensor_scalar(
+                out=k_f[b][:, jb * 512 + c0 : jb * 512 + c0 + n], in0=acc[j][:, c0 : c0 + n],
+                scalar1=EPS, scalar2=None, op0=ALU.max, op1=ALU.add,
+                accum_out=asum[b][:, jb + c0 // 256 : jb + c0 // 256 + 1],
+            )
 
         def su_b(j):
             b, jb, cols = where(j)
-            nc.scalar.activation(
-                out=k_hi[b][:, cols], in_=k_f[b][:, cols], func=ACT.Copy,
-                accum_out=asum[b][:, jb : jb + 1],
-            )
+            nc.scalar.copy(out=k_hi[b][:, cols], in_=k_f[b][:, cols])
 
         def su_c(j):
             b, jb, cols = where(j)
@@ -233,7 +201,7 @@ def tile_sinkhornrouter_kernel(tc, x, w_gate, out):
 
         def su_t(j):
             b, jb, cols = where(j)
-            kt[j] = bank(7, [P, 512], "kt")
+            kt[j] = bank(2 if j == NU // 2 - 1 else 7, [P, 512], "kt")
             for tl in range(4):
                 c0 = jb * 512 + tl * P
                 nc.tensor.transpose(kt[j][:, tl * P : (tl + 1) * P], k_f[b][:, c0 : c0 + P], ident[:])
@@ -324,7 +292,15 @@ def tile_sinkhornrouter_kernel(tc, x, w_gate, out):
             if "t" not in dummy:
                 dummy["t"] = bank(5, [P, 512], "idle")
             for q in range(n):
-                zero_pass(dummy["t"][:], 512, True, True)
+                nc.tensor.matmul_mx(
+                    out=dummy["t"][:],
+                    lhsT=w_codes[:, 0:E].bitcast(FP8X4),
+                    lhsT_scale=w_scales[:, 0:E],
+                    rhs=xc[NU - 1][:, 0:512].bitcast(FP8X4),
+                    rhs_scale=xs[NU - 1][:, 0:512],
+                    start=True,
+                    stop=True,
+                )
 
         fin = {}
         k3 = [k_f[b][:].rearrange("p (t e) -> p t e", e=E) for b in range(NB)]
@@ -368,55 +344,61 @@ def tile_sinkhornrouter_kernel(tc, x, w_gate, out):
             )
 
         for i in range(NU):
-            even = i % 2 == 0 and i >= 2
+            even = i % 2 == 0 and i >= 4
             odd = i % 2 == 1 and i >= 3
-            j = (i - 2) // 2
+            last = i == NU - 1
+            j = (i - 3) // 2 if i % 2 == 1 else (i - 4) // 2
             for g in range(PASSES):
                 transposes(i, g)
                 if g == 0 and i >= 1:
                     quantise(i - 1, 6, 2)
                 if g == 0 and odd:
-                    su_f(j)
-                    su_c(j)
-                if g == 1:
+                    su_a(j, 0, 512)
+                if g == 2:
                     quantise(i, 0, 2)
-                if g == 3 and i == 0:
-                    zero_pass(warm[:], 512, True, True)
+                if g == 4 and odd and not last:
+                    su_b(j)
+                if g == 2 and even:
+                    su_f(j)
                 if g == 3 and i >= 1:
-                    passes(i - 1, 4, 4)
-                if g == 3 and even:
-                    su_a(j)
-                if g == 3 and odd:
-                    su_g(j)
-                if g == 3 and i == 10:
+                    passes(i - 1, 0, 4)
+                if g == 3 and i == 11:
                     v_part(0, 0)
                 if g == 3:
                     quantise(i, 2, 2)
-                if g == 5 and even:
-                    su_b(j)
+                if g == 3 and even:
+                    su_g(j)
+                if g == 5 and odd and not last:
+                    su_c(j)
                 if g == 6:
                     quantise(i, 4, 2)
-                if g == 7 and even:
+                if g == 7 and odd:
                     su_t(j)
-                if g == 7:
-                    passes(i, 0, 4)
+                if g == 7 and i >= 1:
+                    passes(i - 1, 4, 4)
             if i + XBUFS < NU:
                 load(i + XBUFS)
 
         JL = NU // 2 - 1
-        pe_part(0, 1)
+        passes(NU - 1, 0, 4)
+        su_b(JL - 1)
         quantise(NU - 1, 6, 2)
+        pe_part(0, 1)
         passes(NU - 1, 4, 4)
+        dummies(2)
+        su_c(JL - 1)
         v_part(0, 1)
         pe_part(0, 2)
-        su_a(JL)
-        su_b(JL)
+        su_a(JL, 0, 512)
         su_t(JL)
-        dummies(2)
+        dummies(1)
         v_part(1, 0)
+        su_b(JL)
+        su_f(JL - 1)
         su_c(JL)
-        su_f(JL)
         v_part(0, 2)
+        su_g(JL - 1)
+        su_f(JL)
         su_g(JL)
 
         for k in range(1, HALF_STEPS - LEAD):

@@ -30,6 +30,7 @@ NP = 13
 WS = NP + 1
 NDUMMY = 1
 NDUMMY_LONE = 1
+HEAD = {(0, 1): 2, (0, 3): 2, (0, 7): 2}
 LEAD = 2
 HALF_STEPS = 16
 FLOPS = 2 * NB * NTOK * D * E
@@ -68,7 +69,7 @@ def tile_sinkhornrouter_kernel(tc, x, w_gate, out):
         def load(i):
             b, j2 = divmod(i, UNITS_B)
             x_sb[i] = xpool.tile([P, UNIT_T * D], BF16, name="x_sb")
-            if i < NU - 1:
+            if i < NU:
                 nc.sync.dma_start(
                     out=x_sb[i][:],
                     in_=x_flat[b][:, j2 * UNIT_T * D : (j2 + 1) * UNIT_T * D],
@@ -126,6 +127,20 @@ def tile_sinkhornrouter_kernel(tc, x, w_gate, out):
             nc.vector.quantize_mx(
                 out=w_codes[:].bitcast(FP8X4), scales=w_scales[:], in_=wgrp[:]
             )
+
+        warm = bank(6, [P, 512], "warm")
+
+        def w_pass(n):
+            for q in range(n):
+                nc.tensor.matmul_mx(
+                    out=warm[:],
+                    lhsT=w_codes[:, 0:E].bitcast(FP8X4),
+                    lhsT_scale=w_scales[:, 0:E],
+                    rhs=w_codes[:, 0:512].bitcast(FP8X4),
+                    rhs_scale=w_scales[:, 0:512],
+                    start=True,
+                    stop=True,
+                )
 
         def transposes(i, g):
             k = i * PASSES + g + 4
@@ -350,6 +365,7 @@ def tile_sinkhornrouter_kernel(tc, x, w_gate, out):
             j = (i - 3) // 2 if i % 2 == 1 else (i - 4) // 2
             for g in range(PASSES):
                 transposes(i, g)
+                w_pass(HEAD.get((i, g), 0))
                 if g == 0 and i >= 1:
                     quantise(i - 1, 6, 2)
                 if g == 0 and odd:
@@ -368,7 +384,7 @@ def tile_sinkhornrouter_kernel(tc, x, w_gate, out):
                     quantise(i, 2, 2)
                 if g == 3 and even:
                     su_g(j)
-                if g == 5 and odd and not last:
+                if g == 6 and odd and not last:
                     su_c(j)
                 if g == 6:
                     quantise(i, 4, 2)

@@ -30,7 +30,7 @@ NP = 13
 WS = NP + 1
 NDUMMY = 1
 NDUMMY_LONE = 1
-HEAD = {(0, 1): 2, (0, 3): 2, (0, 7): 2}
+BOTH = (1, 2, 3, 8)
 LEAD = 2
 HALF_STEPS = 16
 FLOPS = 2 * NB * NTOK * D * E
@@ -69,7 +69,7 @@ def tile_sinkhornrouter_kernel(tc, x, w_gate, out):
         def load(i):
             b, j2 = divmod(i, UNITS_B)
             x_sb[i] = xpool.tile([P, UNIT_T * D], BF16, name="x_sb")
-            if i < NU:
+            if i < NU - 1:
                 nc.sync.dma_start(
                     out=x_sb[i][:],
                     in_=x_flat[b][:, j2 * UNIT_T * D : (j2 + 1) * UNIT_T * D],
@@ -127,20 +127,6 @@ def tile_sinkhornrouter_kernel(tc, x, w_gate, out):
             nc.vector.quantize_mx(
                 out=w_codes[:].bitcast(FP8X4), scales=w_scales[:], in_=wgrp[:]
             )
-
-        warm = bank(6, [P, 512], "warm")
-
-        def w_pass(n):
-            for q in range(n):
-                nc.tensor.matmul_mx(
-                    out=warm[:],
-                    lhsT=w_codes[:, 0:E].bitcast(FP8X4),
-                    lhsT_scale=w_scales[:, 0:E],
-                    rhs=w_codes[:, 0:512].bitcast(FP8X4),
-                    rhs_scale=w_scales[:, 0:512],
-                    start=True,
-                    stop=True,
-                )
 
         def transposes(i, g):
             k = i * PASSES + g + 4
@@ -365,7 +351,6 @@ def tile_sinkhornrouter_kernel(tc, x, w_gate, out):
             j = (i - 3) // 2 if i % 2 == 1 else (i - 4) // 2
             for g in range(PASSES):
                 transposes(i, g)
-                w_pass(HEAD.get((i, g), 0))
                 if g == 0 and i >= 1:
                     quantise(i - 1, 6, 2)
                 if g == 0 and odd:
@@ -384,7 +369,7 @@ def tile_sinkhornrouter_kernel(tc, x, w_gate, out):
                     quantise(i, 2, 2)
                 if g == 3 and even:
                     su_g(j)
-                if g == 6 and odd and not last:
+                if g == 5 and odd and not last:
                     su_c(j)
                 if g == 6:
                     quantise(i, 4, 2)
@@ -422,7 +407,8 @@ def tile_sinkhornrouter_kernel(tc, x, w_gate, out):
             pe_part(1, k)
             dummies(NDUMMY)
             pe_part(0, k0)
-            dummies(NDUMMY)
+            if k in BOTH:
+                dummies(NDUMMY)
             v_part(1, k)
             v_part(0, k0)
             if k0 == HALF_STEPS - 2:

@@ -26,11 +26,11 @@ UNITS_B = T // UNIT_T
 NU = NB * UNITS_B
 XBUFS = 6
 RING = 5
-NP = 13
-WS = NP + 1
-NDUMMY = 1
+R_B = 6
+R_A = 7
+IDLE = 256
+KICK = (1, 2)
 NDUMMY_LONE = 1
-BOTH = (1, 2, 3, 8)
 LEAD = 2
 HALF_STEPS = 16
 FLOPS = 2 * NB * NTOK * D * E
@@ -90,17 +90,13 @@ def tile_sinkhornrouter_kernel(tc, x, w_gate, out):
         asum = [sink.tile([P, 4], F32, name="asum%d" % b) for b in range(NB)]
         s_v = [sink.tile([P, 1], F32, name="s_v%d" % b) for b in range(NB)]
         v_f = [sink.tile([P, 1], F32, name="v_f%d" % b) for b in range(NB)]
-        v_l = [sink.tile([P, WS], BF16, name="v_l%d" % b) for b in range(NB)]
-        v_h = [sink.tile([P, WS], BF16, name="v_h%d" % b) for b in range(NB)]
+        v_m = [sink.tile([P, 4], BF16, name="v_m%d" % b) for b in range(NB)]
         s_u = [sink.tile([P, T], F32, name="s_u%d" % b) for b in range(NB)]
         u_f = [sink.tile([P, T], F32, name="u_f%d" % b) for b in range(NB)]
-        u_l = [sink.tile([P, T, WS], BF16, name="u_l%d" % b) for b in range(NB)]
-        u_h = [sink.tile([P, T, WS], BF16, name="u_h%d" % b) for b in range(NB)]
+        u_m = [sink.tile([P, T, 4], BF16, name="u_m%d" % b) for b in range(NB)]
         for b in range(NB):
-            nc.vector.memset(v_l[b][:], 0.0)
-            nc.vector.memset(v_h[b][:], 0.0)
-            nc.vector.memset(u_l[b][:], 0.0)
-            nc.vector.memset(u_h[b][:], 0.0)
+            nc.vector.memset(v_m[b][:], 0.0)
+            nc.vector.memset(u_m[b][:], 0.0)
 
         with tc.tile_pool(name="wtmp", bufs=1) as wtmp:
             w_sb = wtmp.tile([P, D], BF16, name="w_sb")
@@ -222,38 +218,45 @@ def tile_sinkhornrouter_kernel(tc, x, w_gate, out):
         FIN = ((2, 6, 7, 3), (4, 1, 2, 6))
         ps = {}
 
-        def thin(dst, part, t, rhs, start, stop):
+        def thin(dst, part, t, pair, r, start, stop):
             nc.tensor.matmul(
-                out=dst, lhsT=part[:, t * P : (t + 1) * P], rhs=rhs, start=start, stop=stop
+                out=dst.rearrange("p (r c) -> p r c", c=2),
+                lhsT=part[:, t * P : (t + 1) * P],
+                rhs=pair.unsqueeze(1).to_broadcast([P, r, 2]),
+                start=start,
+                stop=stop,
             )
 
         def late(b, k):
             return range(12, T) if (b == 1 and k == 1) else range(0)
 
+        NB_ = 2 * R_B
+        NA_ = 2 * R_A
+
         def pe_lo(b, k):
             if k % 2 == 1:
-                pb = bank(BANK_B[b], [P, T, 2 * NP], "ps_b")
+                pb = bank(BANK_B[b], [P, T, 2 * NB_], "ps_b")
                 ps[("b", b)] = pb
                 for t in range(T):
                     if t not in late(b, k):
-                        thin(pb[:, t, 0:NP], k_lo[b], t, v_l[b][:, 0:NP], True, True)
+                        thin(pb[:, t, 0:NB_], k_lo[b], t, v_m[b][:, 0:2], R_B, True, True)
             else:
-                pa = bank(BANK_A[b], [P, 2 * NP], "ps_a")
+                pa = bank(BANK_A[b], [P, 2 * NA_], "ps_a")
                 ps[("a", b)] = pa
                 for t in range(T):
-                    thin(pa[:, 0:NP], kt_lo[b], t, u_l[b][:, t, 0:NP], t == 0, t == T - 1)
+                    thin(pa[:, 0:NA_], kt_lo[b], t, u_m[b][:, t, 0:2], R_A, t == 0, t == T - 1)
 
         def pe_hi(b, k):
             if k % 2 == 1:
                 pb = ps[("b", b)]
                 for t in range(T):
-                    thin(pb[:, t, NP : 2 * NP], k_hi[b], t, v_h[b][:, 0:NP], True, True)
+                    thin(pb[:, t, NB_ : 2 * NB_], k_hi[b], t, v_m[b][:, 1:3], R_B, True, True)
                 for t in late(b, k):
-                    thin(pb[:, t, 0:NP], k_lo[b], t, v_l[b][:, 0:NP], True, True)
+                    thin(pb[:, t, 0:NB_], k_lo[b], t, v_m[b][:, 0:2], R_B, True, True)
             else:
                 pa = ps[("a", b)]
                 for t in range(T):
-                    thin(pa[:, NP : 2 * NP], kt_hi[b], t, u_h[b][:, t, 0:NP], t == 0, t == T - 1)
+                    thin(pa[:, NA_ : 2 * NA_], kt_hi[b], t, u_m[b][:, t, 1:3], R_A, t == 0, t == T - 1)
 
         def pe_part(b, k):
             pe_lo(b, k)
@@ -265,40 +268,37 @@ def tile_sinkhornrouter_kernel(tc, x, w_gate, out):
                     nc.vector.tensor_reduce(out=s_v[b][:], in_=asum[b][:], axis=AX.X, op=ALU.add)
                     first = s_v[b][:]
                 else:
-                    first = ps[("a", b)][:, NP : NP + 1]
+                    first = ps[("a", b)][:, NA_ : NA_ + 1]
                 total, full = s_v[b][:], v_f[b][:]
-                hi_l, hi_h, lo_h = v_l[b][:, NP - 1 : NP], v_h[b][:, 0:1], v_h[b][:, 1:2]
-                whole = None if k == 0 else ps[("a", b)][:, NP - 1 : NP + 2]
+                hi, lo = v_m[b][:, 1:2], v_m[b][:, 2:3]
+                whole = None if k == 0 else ps[("a", b)][:, NA_ - 1 : NA_ + 2]
             else:
-                first = ps[("b", b)][:, :, NP]
+                first = ps[("b", b)][:, :, NB_]
                 total, full = s_u[b][:], u_f[b][:]
-                hi_l, hi_h, lo_h = u_l[b][:, :, NP - 1], u_h[b][:, :, 0], u_h[b][:, :, 1]
-                whole = ps[("b", b)][:, :, NP - 1 : NP + 2]
+                hi, lo = u_m[b][:, :, 1], u_m[b][:, :, 2]
+                whole = ps[("b", b)][:, :, NB_ - 1 : NB_ + 2]
             last = k == HALF_STEPS - 1
             if whole is not None:
                 nc.vector.tensor_reduce(out=total, in_=whole, axis=AX.X, op=ALU.add)
             if not last:
                 with nc.allow_low_precision(reason="upper term of a two-term bf16 split"):
-                    nc.vector.reciprocal(out=hi_l, in_=first)
+                    nc.vector.reciprocal(out=hi, in_=first)
             nc.vector.reciprocal(out=full, in_=total)
             if not last:
-                nc.vector.tensor_copy(out=hi_h, in_=hi_l)
-                nc.vector.tensor_tensor(out=lo_h, in0=full, in1=hi_l, op=ALU.subtract)
+                nc.vector.tensor_tensor(out=lo, in0=full, in1=hi, op=ALU.subtract)
 
         dummy = {}
 
-        def dummies(n):
-            if n == 0:
-                return
+        def dummies(n, width=512):
             if "t" not in dummy:
                 dummy["t"] = bank(5, [P, 512], "idle")
             for q in range(n):
                 nc.tensor.matmul_mx(
-                    out=dummy["t"][:],
+                    out=dummy["t"][:, 0:width],
                     lhsT=w_codes[:, 0:E].bitcast(FP8X4),
                     lhsT_scale=w_scales[:, 0:E],
-                    rhs=xc[NU - 1][:, 0:512].bitcast(FP8X4),
-                    rhs_scale=xs[NU - 1][:, 0:512],
+                    rhs=w_codes[:, 0:width].bitcast(FP8X4),
+                    rhs_scale=w_scales[:, 0:width],
                     start=True,
                     stop=True,
                 )
@@ -405,10 +405,9 @@ def tile_sinkhornrouter_kernel(tc, x, w_gate, out):
         for k in range(1, HALF_STEPS - LEAD):
             k0 = k + LEAD
             pe_part(1, k)
-            dummies(NDUMMY)
+            dummies(1, 512 if k in KICK else IDLE)
             pe_part(0, k0)
-            if k in BOTH:
-                dummies(NDUMMY)
+            dummies(1 if k in KICK else 0)
             v_part(1, k)
             v_part(0, k0)
             if k0 == HALF_STEPS - 2:

@@ -87,7 +87,7 @@ def tile_sinkhornrouter_kernel(tc, x, w_gate, out):
         k_lo = [sink.tile([P, NTOK], BF16, name="k_lo%d" % b) for b in range(NB)]
         kt_hi = [sink.tile([P, NTOK], BF16, name="kt_hi%d" % b) for b in range(NB)]
         kt_lo = [sink.tile([P, NTOK], BF16, name="kt_lo%d" % b) for b in range(NB)]
-        asum = [sink.tile([P, 4], F32, name="asum%d" % b) for b in range(NB)]
+        asum = [sink.tile([P, 8], F32, name="asum%d" % b) for b in range(NB)]
         s_v = [sink.tile([P, 1], F32, name="s_v%d" % b) for b in range(NB)]
         v_f = [sink.tile([P, 1], F32, name="v_f%d" % b) for b in range(NB)]
         v_m = [sink.tile([P, 4], BF16, name="v_m%d" % b) for b in range(NB)]
@@ -97,6 +97,7 @@ def tile_sinkhornrouter_kernel(tc, x, w_gate, out):
         for b in range(NB):
             nc.vector.memset(v_m[b][:], 0.0)
             nc.vector.memset(u_m[b][:], 0.0)
+            nc.vector.memset(asum[b][:], 0.0)
 
         with tc.tile_pool(name="wtmp", bufs=1) as wtmp:
             w_sb = wtmp.tile([P, D], BF16, name="w_sb")
@@ -183,34 +184,39 @@ def tile_sinkhornrouter_kernel(tc, x, w_gate, out):
             nc.vector.tensor_scalar(
                 out=k_f[b][:, jb * 512 + c0 : jb * 512 + c0 + n], in0=acc[j][:, c0 : c0 + n],
                 scalar1=EPS, scalar2=None, op0=ALU.max, op1=ALU.add,
-                accum_out=asum[b][:, jb + c0 // 256 : jb + c0 // 256 + 1],
+                accum_out=asum[b][:, 2 * jb + c0 // 256 : 2 * jb + c0 // 256 + 1],
             )
 
-        def su_b(j):
+        def su_b(j, c0=0, n=512):
             b, jb, cols = where(j)
+            cols = slice(jb * 512 + c0, jb * 512 + c0 + n)
             nc.scalar.copy(out=k_hi[b][:, cols], in_=k_f[b][:, cols])
 
-        def su_c(j):
+        def su_c(j, c0=0, n=512):
             b, jb, cols = where(j)
+            cols = slice(jb * 512 + c0, jb * 512 + c0 + n)
             nc.vector.tensor_tensor(
                 out=k_lo[b][:, cols], in0=k_f[b][:, cols], in1=k_hi[b][:, cols], op=ALU.subtract
             )
 
-        def su_t(j):
+        def su_t(j, t0=0, n=4):
             b, jb, cols = where(j)
-            kt[j] = bank(2 if j == NU // 2 - 1 else 7, [P, 512], "kt")
-            for tl in range(4):
+            if t0 == 0:
+                kt[j] = bank(2 if j == NU // 2 - 1 else 7, [P, 512], "kt")
+            for tl in range(t0, t0 + n):
                 c0 = jb * 512 + tl * P
                 nc.tensor.transpose(kt[j][:, tl * P : (tl + 1) * P], k_f[b][:, c0 : c0 + P], ident[:])
 
-        def su_f(j):
+        def su_f(j, c0=0, n=512):
             b, jb, cols = where(j)
-            nc.scalar.copy(out=kt_hi[b][:, cols], in_=kt[j][:])
+            cols = slice(jb * 512 + c0, jb * 512 + c0 + n)
+            nc.scalar.copy(out=kt_hi[b][:, cols], in_=kt[j][:, c0 : c0 + n])
 
-        def su_g(j):
+        def su_g(j, c0=0, n=512):
             b, jb, cols = where(j)
+            cols = slice(jb * 512 + c0, jb * 512 + c0 + n)
             nc.vector.tensor_tensor(
-                out=kt_lo[b][:, cols], in0=kt[j][:], in1=kt_hi[b][:, cols], op=ALU.subtract
+                out=kt_lo[b][:, cols], in0=kt[j][:, c0 : c0 + n], in1=kt_hi[b][:, cols], op=ALU.subtract
             )
 
         BANK_B = (3, 0)
@@ -227,65 +233,67 @@ def tile_sinkhornrouter_kernel(tc, x, w_gate, out):
                 stop=stop,
             )
 
-        def late(b, k):
-            return range(12, T) if (b == 1 and k == 1) else range(0)
-
         NB_ = 2 * R_B
         NA_ = 2 * R_A
 
-        def pe_lo(b, k):
+        def pe_open(b, k):
             if k % 2 == 1:
-                pb = bank(BANK_B[b], [P, T, 2 * NB_], "ps_b")
-                ps[("b", b)] = pb
-                for t in range(T):
-                    if t not in late(b, k):
-                        thin(pb[:, t, 0:NB_], k_lo[b], t, v_m[b][:, 0:2], R_B, True, True)
+                ps[("b", b)] = bank(BANK_B[b], [P, T, 2 * NB_], "ps_b")
             else:
-                pa = bank(BANK_A[b], [P, 2 * NA_], "ps_a")
-                ps[("a", b)] = pa
-                for t in range(T):
-                    thin(pa[:, 0:NA_], kt_lo[b], t, u_m[b][:, t, 0:2], R_A, t == 0, t == T - 1)
+                ps[("a", b)] = bank(BANK_A[b], [P, 2 * NA_], "ps_a")
 
-        def pe_hi(b, k):
-            if k % 2 == 1:
-                pb = ps[("b", b)]
-                for t in range(T):
-                    thin(pb[:, t, NB_ : 2 * NB_], k_hi[b], t, v_m[b][:, 1:3], R_B, True, True)
-                for t in late(b, k):
-                    thin(pb[:, t, 0:NB_], k_lo[b], t, v_m[b][:, 0:2], R_B, True, True)
-            else:
-                pa = ps[("a", b)]
-                for t in range(T):
-                    thin(pa[:, NA_ : 2 * NA_], kt_hi[b], t, u_m[b][:, t, 1:3], R_A, t == 0, t == T - 1)
+        def pe_lo(b, k, ts=range(T)):
+            for t in ts:
+                if k % 2 == 1:
+                    thin(ps[("b", b)][:, t, 0:NB_], k_lo[b], t, v_m[b][:, 0:2], R_B, True, True)
+                else:
+                    thin(ps[("a", b)][:, 0:NA_], kt_lo[b], t, u_m[b][:, t, 0:2], R_A, t == 0, t == T - 1)
+
+        def pe_hi(b, k, ts=range(T)):
+            for t in ts:
+                if k % 2 == 1:
+                    thin(ps[("b", b)][:, t, NB_ : 2 * NB_], k_hi[b], t, v_m[b][:, 1:3], R_B, True, True)
+                else:
+                    thin(ps[("a", b)][:, NA_ : 2 * NA_], kt_hi[b], t, u_m[b][:, t, 1:3], R_A, t == 0, t == T - 1)
 
         def pe_part(b, k):
+            pe_open(b, k)
             pe_lo(b, k)
             pe_hi(b, k)
 
-        def v_part(b, k):
+        def v_terms(b, k, t0, t1):
             if k % 2 == 0:
-                if k == 0:
-                    nc.vector.tensor_reduce(out=s_v[b][:], in_=asum[b][:], axis=AX.X, op=ALU.add)
-                    first = s_v[b][:]
-                else:
-                    first = ps[("a", b)][:, NA_ : NA_ + 1]
-                total, full = s_v[b][:], v_f[b][:]
                 hi, lo = v_m[b][:, 1:2], v_m[b][:, 2:3]
-                whole = None if k == 0 else ps[("a", b)][:, NA_ - 1 : NA_ + 2]
-            else:
-                first = ps[("b", b)][:, :, NB_]
-                total, full = s_u[b][:], u_f[b][:]
-                hi, lo = u_m[b][:, :, 1], u_m[b][:, :, 2]
-                whole = ps[("b", b)][:, :, NB_ - 1 : NB_ + 2]
-            last = k == HALF_STEPS - 1
-            if whole is not None:
-                nc.vector.tensor_reduce(out=total, in_=whole, axis=AX.X, op=ALU.add)
-            if not last:
+                if k == 0:
+                    return asum[b][:], s_v[b][:], s_v[b][:], v_f[b][:], hi, lo
+                a = ps[("a", b)]
+                return a[:, NA_ - 1 : NA_ + 2], a[:, NA_ : NA_ + 1], s_v[b][:], v_f[b][:], hi, lo
+            a = ps[("b", b)]
+            return (
+                a[:, t0:t1, NB_ - 1 : NB_ + 2], a[:, t0:t1, NB_], s_u[b][:, t0:t1], u_f[b][:, t0:t1],
+                u_m[b][:, t0:t1, 1], u_m[b][:, t0:t1, 2],
+            )
+
+        def v_1(b, k, t0=0, t1=T):
+            whole, first, total, full, hi, lo = v_terms(b, k, t0, t1)
+            nc.vector.tensor_reduce(out=total, in_=whole, axis=AX.X, op=ALU.add)
+            if k < HALF_STEPS - 1:
                 with nc.allow_low_precision(reason="upper term of a two-term bf16 split"):
                     nc.vector.reciprocal(out=hi, in_=first)
+
+        def v_2(b, k, t0=0, t1=T):
+            whole, first, total, full, hi, lo = v_terms(b, k, t0, t1)
             nc.vector.reciprocal(out=full, in_=total)
-            if not last:
-                nc.vector.tensor_tensor(out=lo, in0=full, in1=hi, op=ALU.subtract)
+
+        def v_3(b, k):
+            whole, first, total, full, hi, lo = v_terms(b, k, 0, T)
+            nc.vector.tensor_tensor(out=lo, in0=full, in1=hi, op=ALU.subtract)
+
+        def v_part(b, k):
+            v_1(b, k)
+            v_2(b, k)
+            if k < HALF_STEPS - 1:
+                v_3(b, k)
 
         dummy = {}
 
@@ -323,19 +331,20 @@ def tile_sinkhornrouter_kernel(tc, x, w_gate, out):
                 c0 = (4 * q + tl) * P
                 nc.tensor.transpose(fin[(b, q)][:, tl, :], k_f[b][:, c0 : c0 + P], ident[:])
 
-        def times_u(b, q, eng):
+        def times_u(b, q, eng, t0=0, n=4):
             if eng == "s":
-                for tl in range(4):
+                for tl in range(t0, t0 + n):
                     t = 4 * q + tl
                     nc.scalar.activation(
                         out=k3[b][:, t, :], in_=fin[(b, q)][:, tl, :], func=ACT.Copy,
                         scale=u_f[b][:, t : t + 1],
                     )
             else:
+                t = 4 * q + t0
                 nc.vector.tensor_tensor(
-                    out=k3[b][:, 4 * q : 4 * q + 4, :],
-                    in0=fin[(b, q)][:],
-                    in1=u_f[b][:, 4 * q : 4 * q + 4].unsqueeze(2).to_broadcast([P, 4, E]),
+                    out=k3[b][:, t : t + n, :],
+                    in0=fin[(b, q)][:, t0 : t0 + n, :],
+                    in1=u_f[b][:, t : t + n].unsqueeze(2).to_broadcast([P, n, E]),
                     op=ALU.mult,
                 )
 
@@ -382,28 +391,52 @@ def tile_sinkhornrouter_kernel(tc, x, w_gate, out):
 
         JL = NU // 2 - 1
         passes(NU - 1, 0, 4)
-        su_b(JL - 1)
         quantise(NU - 1, 6, 2)
         pe_part(0, 1)
+        su_a(JL, 0, 256)
+        su_b(JL - 1)
         passes(NU - 1, 4, 4)
-        dummies(2)
         su_c(JL - 1)
-        v_part(0, 1)
-        pe_part(0, 2)
-        su_a(JL, 0, 512)
-        su_t(JL)
+        v_1(0, 1)
+        su_t(JL, 0, 2)
+        v_2(0, 1)
+        su_a(JL, 256, 256)
+        v_3(0, 1)
         dummies(1)
-        v_part(1, 0)
-        su_b(JL)
+        su_b(JL, 0, 256)
         su_f(JL - 1)
-        su_c(JL)
-        v_part(0, 2)
-        su_g(JL - 1)
+        pe_open(0, 2)
+        pe_lo(0, 2)
+        su_t(JL, 2, 2)
+        su_b(JL, 256, 256)
+        v_1(1, 0)
+        pe_hi(0, 2)
+        v_2(1, 0)
+        su_c(JL, 0, 256)
+        v_3(1, 0)
+        su_c(JL, 256, 256)
         su_f(JL)
+        pe_open(1, 1)
+        pe_lo(1, 1, range(12))
+        pe_hi(1, 1)
+        pe_lo(1, 1, range(12, T))
+        v_1(0, 2)
+        su_g(JL - 1)
+        v_2(0, 2)
+        dummies(1)
+        v_1(1, 1)
+        v_3(0, 2)
+        v_2(1, 1)
+        pe_part(0, 3)
+        dummies(1)
+        v_3(1, 1)
         su_g(JL)
+        v_1(0, 3)
+        v_2(0, 3)
+        v_3(0, 3)
 
-        for k in range(1, HALF_STEPS - LEAD):
-            k0 = k + LEAD
+        for k in range(2, 14):
+            k0 = k + 2
             pe_part(1, k)
             dummies(1, 512 if k in KICK else IDLE)
             pe_part(0, k0)
@@ -411,33 +444,49 @@ def tile_sinkhornrouter_kernel(tc, x, w_gate, out):
             v_part(1, k)
             v_part(0, k0)
             if k0 == HALF_STEPS - 2:
-                for q in range(4):
-                    times_v(0, q, "s")
-
-        pe_part(1, 14)
-        dummies(NDUMMY_LONE)
+                times_v(0, 0, "v")
+                times_v(0, 1, "s")
+                times_v(0, 2, "s")
+                times_v(0, 3, "s")
+        pe_open(1, 14)
+        pe_lo(1, 14)
+        pe_hi(1, 14)
+        dummies(1)
         fin_t(0, 0)
+        fin_t(0, 1)
         v_part(1, 14)
-        times_u(0, 0, "s")
-        store(0, 0, 1)
         times_v(1, 0, "v")
         times_v(1, 1, "v")
-        times_v(1, 2, "s")
-        times_v(1, 3, "s")
-        pe_lo(1, 15)
-        dummies(NDUMMY_LONE)
-        pe_hi(1, 15)
-        for q in range(1, 4):
-            fin_t(0, q)
+        times_u(0, 0, "s")
+        store(0, 0, 1)
+        times_v(1, 2, "v")
+        times_v(1, 3, "v")
         times_u(0, 1, "s")
         store(0, 1, 1)
+        pe_open(1, 15)
+        pe_lo(1, 15)
+        dummies(1)
+        fin_t(0, 2)
+        pe_hi(1, 15, range(8))
+        pe_hi(1, 15, range(8, T))
+        fin_t(0, 3)
         times_u(0, 2, "s")
         store(0, 2, 1)
-        v_part(1, 15)
-        times_u(0, 3, "v")
-        store(0, 3, 1)
         for q in range(4):
             fin_t(1, q)
-        for q in range(4):
-            times_u(1, q, "s" if q == 1 else "v")
-            store(1, q, 1)
+        v_1(1, 15, 0, 8)
+        v_1(1, 15, 8, T)
+        v_2(1, 15, 0, 8)
+        v_2(1, 15, 8, T)
+        times_u(0, 3, "s")
+        store(0, 3, 1)
+        times_u(1, 0, "v", 0, 2)
+        times_u(1, 0, "s", 2, 2)
+        store(1, 0, 1)
+        times_u(1, 1, "v")
+        times_u(1, 2, "s")
+        store(1, 1, 1)
+        store(1, 2, 1)
+        times_u(1, 3, "v", 0, 2)
+        times_u(1, 3, "s", 2, 2)
+        store(1, 3, 1)

@@ -29,8 +29,6 @@ RING = 5
 R_B = 6
 R_A = 7
 IDLE = 256
-KICK = (1, 2)
-NDUMMY_LONE = 1
 LEAD = 2
 HALF_STEPS = 16
 FLOPS = 2 * NB * NTOK * D * E
@@ -382,7 +380,7 @@ def tile_sinkhornrouter_kernel(tc, x, w_gate, out):
                     su_c(j)
                 if g == 6:
                     quantise(i, 4, 2)
-                if g == 7 and odd:
+                if g == 7 and odd and not last:
                     su_t(j)
                 if g == 7 and i >= 1:
                     passes(i - 1, 4, 4)
@@ -396,6 +394,7 @@ def tile_sinkhornrouter_kernel(tc, x, w_gate, out):
         su_a(JL, 0, 256)
         su_b(JL - 1)
         passes(NU - 1, 4, 4)
+        su_t(JL - 1)
         su_c(JL - 1)
         v_1(0, 1)
         su_t(JL, 0, 2)
@@ -438,9 +437,8 @@ def tile_sinkhornrouter_kernel(tc, x, w_gate, out):
         for k in range(2, 14):
             k0 = k + 2
             pe_part(1, k)
-            dummies(1, 512 if k in KICK else IDLE)
+            dummies(1, IDLE)
             pe_part(0, k0)
-            dummies(1 if k in KICK else 0)
             v_part(1, k)
             v_part(0, k0)
             if k0 == HALF_STEPS - 2:
@@ -485,8 +483,7 @@ def tile_sinkhornrouter_kernel(tc, x, w_gate, out):
         store(1, 0, 1)
         times_u(1, 1, "v")
         times_u(1, 2, "s")
-        store(1, 1, 1)
-        store(1, 2, 1)
+        store(1, 1, 2)
         times_u(1, 3, "v", 0, 2)
         times_u(1, 3, "s", 2, 2)
         store(1, 3, 1)

from contextlib import ExitStack

import concourse.mybir as mybir
from concourse.masks import make_identity

F32 = mybir.dt.float32
BF16 = mybir.dt.bfloat16
U32 = mybir.dt.uint32
U8 = mybir.dt.uint8
FP8X4 = mybir.dt.float8_e4m3fn_x4
ALU = mybir.AluOpType
ACT = mybir.ActivationFunctionType
AX = mybir.AxisListType

P = 128
NB = 2
NTOK = 2048
D = 4096
E = 128
EPS = 1e-6
T = NTOK // P
PASSES = D // 512
UNIT_T = 2
UNIT_N = UNIT_T * P
UNITS_B = T // UNIT_T
NU = NB * UNITS_B
XBUFS = 6
RING = 5
R_B = 6
R_A = 7
IDLE = 256
LEAD = 2
HALF_STEPS = 16
FLOPS = 2 * NB * NTOK * D * E


def tile_sinkhornrouter_kernel(tc, x, w_gate, out):
    nc = tc.nc
    with ExitStack() as ctx:
        ctx.enter_context(tc.manual_schedule())
        const = ctx.enter_context(tc.tile_pool(name="const", bufs=1))
        psum = ctx.enter_context(tc.psum_pool(name="psum", bufs=1))
        xpool = ctx.enter_context(tc.tile_pool(name="xpool", bufs=XBUFS))
        gpool = ctx.enter_context(tc.tile_pool(name="gpool", bufs=3))
        cpool = ctx.enter_context(tc.tile_pool(name="cpool", bufs=3))
        sink = ctx.enter_context(tc.tile_pool(name="sink", bufs=1))

        def bank(k, shape, name):
            return psum.tile(shape, F32, tag="bank%d" % k, name=name)

        ident = const.tile([P, P], F32, name="ident")
        make_identity(nc, ident[:])
        w_codes = const.tile([P, PASSES * E], U32, name="w_codes", align_bytes=64)
        w_scales = const.tile([P, PASSES * E], U8, name="w_scales", align_bytes=64)

        x_flat = [x[b].rearrange("(p t) d -> p (t d)", t=T) for b in range(NB)]
        x_3d = [x[b].rearrange("(p t) d -> p t d", t=T) for b in range(NB)]
        out_flat = [out[b].rearrange("(p t) e -> p (t e)", t=T) for b in range(NB)]

        x_sb = {}
        grp = {}
        xc = {}
        xs = {}
        acc = {}
        kt = {}

        def load(i):
            b, j2 = divmod(i, UNITS_B)
            x_sb[i] = xpool.tile([P, UNIT_T * D], BF16, name="x_sb")
            if i < NU - 1:
                nc.sync.dma_start(
                    out=x_sb[i][:],
                    in_=x_flat[b][:, j2 * UNIT_T * D : (j2 + 1) * UNIT_T * D],
                )
            else:
                dst = x_sb[i][:].rearrange("p (t d) -> p t d", t=UNIT_T)
                for h in range(2):
                    nc.sync.dma_start(
                        out=dst[:, :, h * (D // 2) : (h + 1) * (D // 2)],
                        in_=x_3d[b][:, j2 * UNIT_T : (j2 + 1) * UNIT_T, h * (D // 2) : (h + 1) * (D // 2)],
                    )

        k_f = [sink.tile([P, NTOK], F32, name="k_f%d" % b) for b in range(NB)]
        k_hi = [sink.tile([P, NTOK], BF16, name="k_hi%d" % b) for b in range(NB)]
        k_lo = [sink.tile([P, NTOK], BF16, name="k_lo%d" % b) for b in range(NB)]
        kt_hi = [sink.tile([P, NTOK], BF16, name="kt_hi%d" % b) for b in range(NB)]
        kt_lo = [sink.tile([P, NTOK], BF16, name="kt_lo%d" % b) for b in range(NB)]
        asum = [sink.tile([P, 8], F32, name="asum%d" % b) for b in range(NB)]
        s_v = [sink.tile([P, 1], F32, name="s_v%d" % b) for b in range(NB)]
        v_f = [sink.tile([P, 1], F32, name="v_f%d" % b) for b in range(NB)]
        v_m = [sink.tile([P, 4], BF16, name="v_m%d" % b) for b in range(NB)]
        s_u = [sink.tile([P, T], F32, name="s_u%d" % b) for b in range(NB)]
        u_f = [sink.tile([P, T], F32, name="u_f%d" % b) for b in range(NB)]
        u_m = [sink.tile([P, T, 4], BF16, name="u_m%d" % b) for b in range(NB)]
        for b in range(NB):
            nc.vector.memset(v_m[b][:], 0.0)
            nc.vector.memset(u_m[b][:], 0.0)
            nc.vector.memset(asum[b][:], 0.0)

        with tc.tile_pool(name="wtmp", bufs=1) as wtmp:
            w_sb = wtmp.tile([P, D], BF16, name="w_sb")
            nc.sync.dma_start(out=w_sb[:], in_=w_gate)
            for i in range(XBUFS):
                load(i)
            ww = w_sb[:].bitcast(F32)
            wgrp = wtmp.tile([P, PASSES * E * 4], BF16, name="wgrp", align_bytes=64)
            wgw = wgrp[:].bitcast(F32).rearrange("p (g e u) -> p g e u", g=PASSES, e=E, u=2)
            for q in range(PASSES // 2):
                wt = bank(q % RING, [P, 2, 2, E], "wt")
                for g2 in range(2):
                    for u in range(2):
                        blk = 2 * (2 * q + g2) + u
                        nc.tensor.transpose(
                            wt[:, g2, u, :], ww[:, blk * P : (blk + 1) * P], ident[:]
                        )
                dst = wgw[:, 2 * q : 2 * q + 2, :, :]
                src = wt[:].rearrange("p g u e -> p g e u")
                if q % 2 == 0:
                    nc.vector.tensor_copy(out=dst, in_=src)
                else:
                    nc.scalar.copy(out=dst, in_=src)
            nc.vector.quantize_mx(
                out=w_codes[:].bitcast(FP8X4), scales=w_scales[:], in_=wgrp[:]
            )

        def transposes(i, g):
            k = i * PASSES + g + 4
            if g % 4 == 0:
                grp[(i, g // 4)] = gpool.tile([P, 4 * UNIT_N * 4], BF16, name="grp", align_bytes=64)
            xt = bank(k % RING, [P, 2, UNIT_N], "xt")
            xw = x_sb[i][:].bitcast(F32)
            for u in range(2):
                for tl in range(UNIT_T):
                    c0 = tl * (D // 2) + 256 * g + P * u
                    nc.tensor.transpose(
                        xt[:, u, tl * P : (tl + 1) * P], xw[:, c0 : c0 + P], ident[:]
                    )
            gw = grp[(i, g // 4)][:].bitcast(F32).rearrange(
                "p (g n u) -> p g n u", g=4, n=UNIT_N, u=2
            )
            src = xt[:].rearrange("p u n -> p n u")
            if g == 6 or (g == 2 and i % 2 == 0):
                nc.vector.tensor_copy(out=gw[:, g % 4, :, :], in_=src)
            else:
                nc.scalar.copy(out=gw[:, g % 4, :, :], in_=src)

        def quantise(i, g0, n):
            if g0 == 0:
                xc[i] = cpool.tile([P, PASSES * UNIT_N], U32, name="xc", align_bytes=64)
                xs[i] = cpool.tile([P, PASSES * UNIT_N], U8, name="xs", align_bytes=64)
            c0 = g0 * UNIT_N
            c1 = (g0 + n) * UNIT_N
            r0 = (g0 % 4) * UNIT_N * 4
            nc.vector.quantize_mx(
                out=xc[i][:, c0:c1].bitcast(FP8X4),
                scales=xs[i][:, c0:c1],
                in_=grp[(i, g0 // 4)][:, r0 : r0 + n * UNIT_N * 4],
            )

        def passes(i, g0, n):
            j = i // 2
            if i % 2 == 0 and g0 == 0:
                acc[j] = bank(RING + j % 2, [P, 2 * UNIT_N], "acc")
            c0 = (i % 2) * UNIT_N
            for g in range(g0, g0 + n):
                nc.tensor.matmul_mx(
                    out=acc[j][:, c0 : c0 + UNIT_N],
                    lhsT=w_codes[:, g * E : (g + 1) * E].bitcast(FP8X4),
                    lhsT_scale=w_scales[:, g * E : (g + 1) * E],
                    rhs=xc[i][:, g * UNIT_N : (g + 1) * UNIT_N].bitcast(FP8X4),
                    rhs_scale=xs[i][:, g * UNIT_N : (g + 1) * UNIT_N],
                    start=(g == 0),
                    stop=(g == PASSES - 1),
                )

        def where(j):
            b, jb = divmod(j, 4)
            return b, jb, slice(jb * 512, (jb + 1) * 512)

        def su_a(j, c0, n):
            b, jb, cols = where(j)
            nc.vector.tensor_scalar(
                out=k_f[b][:, jb * 512 + c0 : jb * 512 + c0 + n], in0=acc[j][:, c0 : c0 + n],
                scalar1=EPS, scalar2=None, op0=ALU.max, op1=ALU.add,
                accum_out=asum[b][:, 2 * jb + c0 // 256 : 2 * jb + c0 // 256 + 1],
            )

        def su_b(j, c0=0, n=512):
            b, jb, cols = where(j)
            cols = slice(jb * 512 + c0, jb * 512 + c0 + n)
            nc.scalar.copy(out=k_hi[b][:, cols], in_=k_f[b][:, cols])

        def su_c(j, c0=0, n=512):
            b, jb, cols = where(j)
            cols = slice(jb * 512 + c0, jb * 512 + c0 + n)
            nc.vector.tensor_tensor(
                out=k_lo[b][:, cols], in0=k_f[b][:, cols], in1=k_hi[b][:, cols], op=ALU.subtract
            )

        def su_t(j, t0=0, n=4):
            b, jb, cols = where(j)
            if t0 == 0:
                kt[j] = bank(2 if j == NU // 2 - 1 else 7, [P, 512], "kt")
            for tl in range(t0, t0 + n):
                c0 = jb * 512 + tl * P
                nc.tensor.transpose(kt[j][:, tl * P : (tl + 1) * P], k_f[b][:, c0 : c0 + P], ident[:])

        def su_f(j, c0=0, n=512):
            b, jb, cols = where(j)
            cols = slice(jb * 512 + c0, jb * 512 + c0 + n)
            nc.scalar.copy(out=kt_hi[b][:, cols], in_=kt[j][:, c0 : c0 + n])

        def su_g(j, c0=0, n=512):
            b, jb, cols = where(j)
            cols = slice(jb * 512 + c0, jb * 512 + c0 + n)
            nc.vector.tensor_tensor(
                out=kt_lo[b][:, cols], in0=kt[j][:, c0 : c0 + n], in1=kt_hi[b][:, cols], op=ALU.subtract
            )

        BANK_B = (3, 0)
        BANK_A = (4, 1)
        FIN = ((2, 6, 7, 3), (4, 1, 2, 6))
        ps = {}

        def thin(dst, part, t, pair, r, start, stop):
            nc.tensor.matmul(
                out=dst.rearrange("p (r c) -> p r c", c=2),
                lhsT=part[:, t * P : (t + 1) * P],
                rhs=pair.unsqueeze(1).to_broadcast([P, r, 2]),
                start=start,
                stop=stop,
            )

        NB_ = 2 * R_B
        NA_ = 2 * R_A

        def pe_open(b, k):
            if k % 2 == 1:
                ps[("b", b)] = bank(BANK_B[b], [P, T, 2 * NB_], "ps_b")
            else:
                ps[("a", b)] = bank(BANK_A[b], [P, 2 * NA_], "ps_a")

        def pe_lo(b, k, ts=range(T)):
            for t in ts:
                if k % 2 == 1:
                    thin(ps[("b", b)][:, t, 0:NB_], k_lo[b], t, v_m[b][:, 0:2], R_B, True, True)
                else:
                    thin(ps[("a", b)][:, 0:NA_], kt_lo[b], t, u_m[b][:, t, 0:2], R_A, t == 0, t == T - 1)

        def pe_hi(b, k, ts=range(T)):
            for t in ts:
                if k % 2 == 1:
                    thin(ps[("b", b)][:, t, NB_ : 2 * NB_], k_hi[b], t, v_m[b][:, 1:3], R_B, True, True)
                else:
                    thin(ps[("a", b)][:, NA_ : 2 * NA_], kt_hi[b], t, u_m[b][:, t, 1:3], R_A, t == 0, t == T - 1)

        def pe_part(b, k):
            pe_open(b, k)
            pe_lo(b, k)
            pe_hi(b, k)

        def v_terms(b, k, t0, t1):
            if k % 2 == 0:
                hi, lo = v_m[b][:, 1:2], v_m[b][:, 2:3]
                if k == 0:
                    return asum[b][:], s_v[b][:], s_v[b][:], v_f[b][:], hi, lo
                a = ps[("a", b)]
                return a[:, NA_ - 1 : NA_ + 2], a[:, NA_ : NA_ + 1], s_v[b][:], v_f[b][:], hi, lo
            a = ps[("b", b)]
            return (
                a[:, t0:t1, NB_ - 1 : NB_ + 2], a[:, t0:t1, NB_], s_u[b][:, t0:t1], u_f[b][:, t0:t1],
                u_m[b][:, t0:t1, 1], u_m[b][:, t0:t1, 2],
            )

        def v_1(b, k, t0=0, t1=T):
            whole, first, total, full, hi, lo = v_terms(b, k, t0, t1)
            nc.vector.tensor_reduce(out=total, in_=whole, axis=AX.X, op=ALU.add)
            if k < HALF_STEPS - 1:
                with nc.allow_low_precision(reason="upper term of a two-term bf16 split"):
                    nc.vector.reciprocal(out=hi, in_=first)

        def v_2(b, k, t0=0, t1=T):
            whole, first, total, full, hi, lo = v_terms(b, k, t0, t1)
            nc.vector.reciprocal(out=full, in_=total)

        def v_3(b, k):
            whole, first, total, full, hi, lo = v_terms(b, k, 0, T)
            nc.vector.tensor_tensor(out=lo, in0=full, in1=hi, op=ALU.subtract)

        def v_part(b, k):
            v_1(b, k)
            v_2(b, k)
            if k < HALF_STEPS - 1:
                v_3(b, k)

        dummy = {}

        def dummies(n, width=512):
            if "t" not in dummy:
                dummy["t"] = bank(5, [P, 512], "idle")
            for q in range(n):
                nc.tensor.matmul_mx(
                    out=dummy["t"][:, 0:width],
                    lhsT=w_codes[:, 0:E].bitcast(FP8X4),
                    lhsT_scale=w_scales[:, 0:E],
                    rhs=w_codes[:, 0:width].bitcast(FP8X4),
                    rhs_scale=w_scales[:, 0:width],
                    start=True,
                    stop=True,
                )

        fin = {}
        k3 = [k_f[b][:].rearrange("p (t e) -> p t e", e=E) for b in range(NB)]

        def times_v(b, q, eng):
            cols = slice(q * 512, (q + 1) * 512)
            if eng == "s":
                nc.scalar.activation(
                    out=k_f[b][:, cols], in_=k_f[b][:, cols], func=ACT.Copy, scale=v_f[b][:, 0:1]
                )
            else:
                nc.vector.tensor_scalar_mul(
                    out=k_f[b][:, cols], in0=k_f[b][:, cols], scalar1=v_f[b][:, 0:1]
                )

        def fin_t(b, q):
            fin[(b, q)] = bank(FIN[b][q], [P, 4, E], "fin")
            for tl in range(4):
                c0 = (4 * q + tl) * P
                nc.tensor.transpose(fin[(b, q)][:, tl, :], k_f[b][:, c0 : c0 + P], ident[:])

        def times_u(b, q, eng, t0=0, n=4):
            if eng == "s":
                for tl in range(t0, t0 + n):
                    t = 4 * q + tl
                    nc.scalar.activation(
                        out=k3[b][:, t, :], in_=fin[(b, q)][:, tl, :], func=ACT.Copy,
                        scale=u_f[b][:, t : t + 1],
                    )
            else:
                t = 4 * q + t0
                nc.vector.tensor_tensor(
                    out=k3[b][:, t : t + n, :],
                    in0=fin[(b, q)][:, t0 : t0 + n, :],
                    in1=u_f[b][:, t : t + n].unsqueeze(2).to_broadcast([P, n, E]),
                    op=ALU.mult,
                )

        def store(b, q, n):
            nc.sync.dma_start(
                out=out_flat[b][:, q * 512 : (q + n) * 512], in_=k_f[b][:, q * 512 : (q + n) * 512]
            )

        for i in range(NU):
            even = i % 2 == 0 and i >= 4
            odd = i % 2 == 1 and i >= 3
            last = i == NU - 1
            j = (i - 3) // 2 if i % 2 == 1 else (i - 4) // 2
            for g in range(PASSES):
                transposes(i, g)
                if g == 0 and i >= 1:
                    quantise(i - 1, 6, 2)
                if g == 0 and odd:
                    su_a(j, 0, 512)
                if g == 2:
                    quantise(i, 0, 2)
                if g == 4 and odd and not last:
                    su_b(j)
                if g == 2 and even:
                    su_f(j)
                if g == 3 and i >= 1:
                    passes(i - 1, 0, 4)
                if g == 3 and i == 11:
                    v_part(0, 0)
                if g == 3:
                    quantise(i, 2, 2)
                if g == 3 and even:
                    su_g(j)
                if g == 5 and odd and not last:
                    su_c(j)
                if g == 6:
                    quantise(i, 4, 2)
                if g == 7 and odd and not last:
                    su_t(j)
                if g == 7 and i >= 1:
                    passes(i - 1, 4, 4)
            if i + XBUFS < NU:
                load(i + XBUFS)

        JL = NU // 2 - 1
        passes(NU - 1, 0, 4)
        quantise(NU - 1, 6, 2)
        pe_part(0, 1)
        su_a(JL, 0, 256)
        su_b(JL - 1)
        passes(NU - 1, 4, 4)
        su_t(JL - 1)
        su_c(JL - 1)
        v_1(0, 1)
        su_t(JL, 0, 2)
        v_2(0, 1)
        su_a(JL, 256, 256)
        v_3(0, 1)
        dummies(1)
        su_b(JL, 0, 256)
        su_f(JL - 1)
        pe_open(0, 2)
        pe_lo(0, 2)
        su_t(JL, 2, 2)
        su_b(JL, 256, 256)
        v_1(1, 0)
        pe_hi(0, 2)
        v_2(1, 0)
        su_c(JL, 0, 256)
        v_3(1, 0)
        su_c(JL, 256, 256)
        su_f(JL)
        pe_open(1, 1)
        pe_lo(1, 1, range(12))
        pe_hi(1, 1)
        pe_lo(1, 1, range(12, T))
        v_1(0, 2)
        su_g(JL - 1)
        v_2(0, 2)
        dummies(1)
        v_1(1, 1)
        v_3(0, 2)
        v_2(1, 1)
        pe_part(0, 3)
        dummies(1)
        v_3(1, 1)
        su_g(JL)
        v_1(0, 3)
        v_2(0, 3)
        v_3(0, 3)

        for k in range(2, 14):
            k0 = k + 2
            pe_part(1, k)
            dummies(1, IDLE)
            pe_part(0, k0)
            v_part(1, k)
            v_part(0, k0)
            if k0 == HALF_STEPS - 2:
                times_v(0, 0, "v")
                times_v(0, 1, "s")
                times_v(0, 2, "s")
                times_v(0, 3, "s")
        pe_open(1, 14)
        pe_lo(1, 14)
        pe_hi(1, 14)
        dummies(1)
        fin_t(0, 0)
        fin_t(0, 1)
        v_part(1, 14)
        times_v(1, 0, "v")
        times_v(1, 1, "v")
        times_u(0, 0, "s")
        store(0, 0, 1)
        times_v(1, 2, "v")
        times_v(1, 3, "v")
        times_u(0, 1, "s")
        store(0, 1, 1)
        pe_open(1, 15)
        pe_lo(1, 15)
        dummies(1)
        fin_t(0, 2)
        pe_hi(1, 15, range(8))
        pe_hi(1, 15, range(8, T))
        fin_t(0, 3)
        times_u(0, 2, "s")
        store(0, 2, 1)
        for q in range(4):
            fin_t(1, q)
        v_1(1, 15, 0, 8)
        v_1(1, 15, 8, T)
        v_2(1, 15, 0, 8)
        v_2(1, 15, 8, T)
        times_u(0, 3, "s")
        store(0, 3, 1)
        times_u(1, 0, "v", 0, 2)
        times_u(1, 0, "s", 2, 2)
        store(1, 0, 1)
        times_u(1, 1, "v")
        times_u(1, 2, "s")
        store(1, 1, 2)
        times_u(1, 3, "v", 0, 2)
        times_u(1, 3, "s", 2, 2)
        store(1, 3, 1)
